import numpy as np
import ml_dtypes


def mxq(x, axis, fmt="e4m3"):
    dtype, down = {"e4m3": (ml_dtypes.float8_e4m3fn, 7), "e5m2": (ml_dtypes.float8_e5m2, 14)}[fmt]
    v = np.moveaxis(np.asarray(x, np.float32).astype(ml_dtypes.bfloat16).astype(np.float64), axis, -1)
    blocks = v.reshape(v.shape[:-1] + (-1, 32))
    amax = np.abs(blocks).max(-1, keepdims=True)
    byte = np.maximum(np.where(amax > 0, np.frexp(amax)[1] - 1 + 127, 0) - down, 1)
    scale = np.exp2(byte - 127.0)
    codes = (blocks / scale).astype(np.float32).astype(dtype).astype(np.float64)
    return np.moveaxis((codes * scale).reshape(v.shape), -1, axis)


WIDE = False


def mx_kscale(k):
    if not WIDE:
        return np.ones(k)
    levels = np.array([10, -10, 5, -5, 0])
    a = np.random.permutation(np.resize(levels, k // 512 * 4)).reshape(k // 512, 4)
    idx = np.arange(k)
    return np.exp2(a[idx // 512, idx % 128 // 32])


BF16 = ml_dtypes.bfloat16


def bf(x):
    return np.asarray(x, np.float32).astype(BF16)


def f64(x):
    return np.asarray(x).astype(np.float64)


B, S, D, A, H = 1, 512, 8192, 1024, 8
HD = A // H


def setup_inputs():
    s = mx_kscale(D)
    return {"q_rot": bf(np.random.standard_normal((B, S, A)) * 1.5 / np.sqrt(HD)),
            "k_rot": bf(np.random.standard_normal((B, S, A)) * 0.5),
            "hidden_states": bf(np.random.standard_normal((B, S, D)) * s),
            "Wv": bf(np.random.standard_normal((A, D)) * 0.5 / np.sqrt(D) / s),
            "bv": bf(np.random.standard_normal(A) * 2.0 * H / S)}


def reference(q_rot, k_rot, hidden_states, Wv, bv):
    v = (mxq(f64(hidden_states), 2, "e4m3") @ mxq(f64(Wv), 1, "e4m3").T) + f64(bv)
    qh = f64(q_rot).reshape(B, S, H, HD).transpose(0, 2, 1, 3)
    kh = f64(k_rot).reshape(B, S, H, HD).transpose(0, 2, 1, 3)
    vh = v.reshape(B, S, H, HD).transpose(0, 2, 1, 3)
    scores = qh @ kh.transpose(0, 1, 3, 2)
    e = np.exp(scores - scores.max(1, keepdims=True))
    probs = e / e.sum(1, keepdims=True)
    ctx = mxq(probs, 3, "e4m3") @ mxq(vh, 2, "e4m3")
    return ctx.reshape(B, S, A)

@@ -1,0 +1,281 @@
+from contextlib import ExitStack
+
+import concourse.mybir as mybir
+from concourse.masks import make_identity
+
+F32 = mybir.dt.float32
+BF16 = mybir.dt.bfloat16
+U32 = mybir.dt.uint32
+U8 = mybir.dt.uint8
+FP8X4 = mybir.dt.float8_e4m3fn_x4
+ALU = mybir.AluOpType
+ACT = mybir.ActivationFunctionType
+AXIS = mybir.AxisListType
+
+P = 128
+PACK = 4
+K_PASS = P * PACK
+S = 512
+D = 8192
+A = 1024
+H = 8
+HD = A // H
+ROW_TILES = S // P
+PASSES = D // K_PASS
+BANK = 512
+RAW = 4096
+HS_STEPS = S * D // (P * RAW)
+WV_STEPS = A * D // (P * RAW)
+STEPS = HS_STEPS + WV_STEPS
+UNITS = ROW_TILES * ROW_TILES
+AHEAD = 3
+
+FLOPS = 2 * S * A * D + 2 * 2 * H * S * S * HD
+
+
+def tile_sparseattention_pb_k_kernel(tc, q_rot, k_rot, hidden_states, Wv, bv, out):
+    nc = tc.nc
+    with ExitStack() as ctx:
+        ctx.enter_context(tc.manual_schedule())
+        keep = ctx.enter_context(tc.tile_pool(name="keep", bufs=1))
+        work = ctx.enter_context(tc.tile_pool(name="work", bufs=2))
+        psum = ctx.enter_context(tc.psum_pool(name="psum", bufs=2))
+
+        q_rows = q_rot.flatten_outer_dims().rearrange("(p t) a -> p t a", t=ROW_TILES)
+        k_rows = k_rot.flatten_outer_dims().rearrange("(p t) a -> p t a", t=ROW_TILES)
+        hs_rows = hidden_states.flatten_outer_dims().rearrange("(p t) k -> p t k", t=ROW_TILES)
+        out_heads = out.flatten_outer_dims().rearrange("(h a) (b x) -> h (a b) x", h=H, b=2)
+
+        ident_f32 = keep.tile([P, P], F32)
+        make_identity(nc, ident_f32[:])
+        ident_bf16 = keep.tile([P, P], BF16)
+        make_identity(nc, ident_bf16[:])
+        bias = keep.tile([P, A], BF16)
+        nc.scalar.dma_start(out=bias[:], in_=bv.partition_broadcast(P))
+
+        qT = keep.tile([P, A * ROW_TILES], BF16)
+        kT = keep.tile([P, A * ROW_TILES], BF16)
+        hs_codes = keep.tile([P, PASSES * S], U32, align_bytes=64)
+        hs_scales = keep.tile([P, PASSES * S], U8, align_bytes=64)
+        p_codes = keep.tile([P, H * S], U32, align_bytes=64)
+        p_scales = keep.tile([P, H * S], U8, align_bytes=64)
+        v_codes = keep.tile([P, A], U32, align_bytes=64)
+        v_scales = keep.tile([P, A], U8, align_bytes=64)
+
+        def load_rows(view):
+            raw = work.tile([P, RAW], BF16, tag="raw", bufs=AHEAD + 2)
+            nc.sync.dma_start(out=raw[:].rearrange("p (t c) -> p t c", t=view.shape[1]), in_=view)
+            return raw
+
+        def load_step(s):
+            if s < HS_STEPS:
+                return load_rows(hs_rows[:, :, s * (RAW // ROW_TILES) : (s + 1) * (RAW // ROW_TILES)])
+            h, half = divmod(s - HS_STEPS, 2)
+            return load_rows(Wv[h * HD : (h + 1) * HD, half * RAW : (half + 1) * RAW].unsqueeze(1))
+
+        def transpose_heads(raw, dst):
+            for pair in range(H // 2):
+                bank = psum.tile([P, 2 * BANK], BF16, tag="tp", bufs=4)
+                for hh in range(2):
+                    for t in range(ROW_TILES):
+                        col = t * A + (2 * pair + hh) * HD
+                        slot = (hh * ROW_TILES + t) * P
+                        nc.tensor.transpose(bank[:, slot : slot + P], raw[:, col : col + HD], ident_bf16[:])
+                copy = nc.scalar.copy if pair % 2 == 0 else nc.vector.tensor_copy
+                copy(out=dst[:, pair * 2 * BANK : (pair + 1) * 2 * BANK], in_=bank[:])
+
+        def transpose_step(s, raw):
+            words = raw[:].bitcast(F32)
+            grouped = work.tile([P, RAW], BF16, tag="grouped", bufs=2, align_bytes=64)
+            grouped_words = grouped[:].bitcast(F32)
+            for b in range(RAW // 2 // BANK):
+                bank = psum.tile([P, BANK], F32, tag="tp", bufs=4)
+                for a in range(2):
+                    for u in range(2):
+                        if s < HS_STEPS:
+                            blk = (2 * (b % 2) + a) * 4 + (b // 2) * 2 + u
+                        else:
+                            blk = 4 * b + 2 * a + u
+                        slot = (2 * a + u) * P
+                        nc.tensor.transpose(bank[:, slot : slot + P], words[:, blk * P : (blk + 1) * P], ident_f32[:])
+                nc.scalar.copy(
+                    out=grouped_words[:, b * BANK : (b + 1) * BANK].rearrange("p (a r u) -> p a r u", a=2, u=2),
+                    in_=bank[:].rearrange("p (a u r) -> p a r u", a=2, u=2),
+                )
+            return grouped
+
+        def quantise_step(s, grouped, w_codes, w_scales):
+            if s < HS_STEPS:
+                cols = slice(s * (RAW // PACK), (s + 1) * (RAW // PACK))
+                nc.vector.quantize_mx(out=hs_codes[:, cols].bitcast(FP8X4), scales=hs_scales[:, cols], in_=grouped[:])
+            else:
+                half = (s - HS_STEPS) % 2
+                cols = slice(half * (RAW // PACK), (half + 1) * (RAW // PACK))
+                nc.vector.quantize_mx(out=w_codes[:, cols].bitcast(FP8X4), scales=w_scales[:, cols], in_=grouped[:])
+
+        def project_groups(acc, first_t, w_codes, w_scales):
+            for t in range(first_t, first_t + 2):
+                for c in range(PASSES):
+                    hs_cols = slice(c * S + t * P, c * S + (t + 1) * P)
+                    w_cols = slice(c * HD, (c + 1) * HD)
+                    nc.tensor.matmul_mx(
+                        out=acc[:, t * HD : (t + 1) * HD],
+                        lhsT=hs_codes[:, hs_cols].bitcast(FP8X4),
+                        lhsT_scale=hs_scales[:, hs_cols],
+                        rhs=w_codes[:, w_cols].bitcast(FP8X4),
+                        rhs_scale=w_scales[:, w_cols],
+                        start=(c == 0),
+                        stop=(c == PASSES - 1),
+                    )
+
+        def quantise_v(h, acc):
+            v_grouped = work.tile([P, HD * PACK], BF16, tag="v_grouped", align_bytes=64)
+            nc.vector.tensor_tensor(
+                out=v_grouped[:].rearrange("p (d t) -> p d t", t=PACK),
+                in0=acc[:].rearrange("p (t d) -> p d t", t=PACK),
+                in1=bias[:, h * HD : (h + 1) * HD].unsqueeze(2).to_broadcast([P, HD, PACK]),
+                op=ALU.add,
+            )
+            cols = slice(h * HD, (h + 1) * HD)
+            nc.vector.quantize_mx(out=v_codes[:, cols].bitcast(FP8X4), scales=v_scales[:, cols], in_=v_grouped[:])
+
+        expd = {}
+        inverse = {}
+        totals = {}
+
+        def scores_minus_max(it, t):
+            if t == 0:
+                expd[it] = work.tile([P, ROW_TILES * A], F32, tag="expd", name="expd")
+                inverse[it] = work.tile([P, P * PACK], F32, tag="inverse", name="inverse")
+            banks = []
+            for g in range(2):
+                sc = psum.tile([P, BANK], F32, tag="sc", bufs=2, name="sc")
+                for hh in range(H // 2):
+                    h = g * (H // 2) + hh
+                    nc.tensor.matmul(
+                        out=sc[:, hh * P : (hh + 1) * P],
+                        lhsT=kT[:, h * S + t * P : h * S + (t + 1) * P],
+                        rhs=qT[:, h * S + it * P : h * S + (it + 1) * P],
+                        start=True,
+                        stop=True,
+                    )
+                banks.append(sc)
+            half_max = work.tile([P, 2 * P], F32, tag="half_max")
+            for g in range(2):
+                nc.vector.tensor_reduce(
+                    out=half_max[:, g * P : (g + 1) * P],
+                    in_=banks[g][:].rearrange("p (h i) -> p i h", h=H // 2),
+                    axis=AXIS.X,
+                    op=ALU.max,
+                )
+            top = work.tile([P, P], F32, tag="top")
+            nc.vector.tensor_tensor(out=top[:], in0=half_max[:, 0:P], in1=half_max[:, P : 2 * P], op=ALU.max)
+            for g in range(2):
+                first = t * A + g * BANK
+                nc.vector.tensor_tensor(
+                    out=expd[it][:, first : first + BANK].rearrange("p (h i) -> p h i", h=H // 2),
+                    in0=banks[g][:].rearrange("p (h i) -> p h i", h=H // 2),
+                    in1=top[:].unsqueeze(1).to_broadcast([P, H // 2, P]),
+                    op=ALU.subtract,
+                )
+
+        def exp_and_sum(it, t):
+            unit_cols = expd[it][:, t * A : (t + 1) * A]
+            nc.scalar.activation(out=unit_cols, in_=unit_cols, func=ACT.Exp)
+            part = work.tile([P, 4 * P], F32, tag="part")
+            nc.gpsimd.tensor_tensor(out=part[:], in0=unit_cols[:, 0 : 4 * P], in1=unit_cols[:, 4 * P : 8 * P], op=ALU.add)
+            nc.gpsimd.tensor_tensor(out=part[:, 0 : 2 * P], in0=part[:, 0 : 2 * P], in1=part[:, 2 * P : 4 * P], op=ALU.add)
+            totals[t] = work.tile([P, P], F32, tag="total", name="total")
+            nc.gpsimd.tensor_tensor(out=totals[t][:], in0=part[:, 0:P], in1=part[:, P : 2 * P], op=ALU.add)
+
+        def invert_sum(it, t):
+            nc.vector.reciprocal(out=inverse[it][:].rearrange("p (i t) -> p i t", t=PACK)[:, :, t], in_=totals[t][:])
+
+        p_grouped = {}
+
+        def normalise_head(it, h):
+            if h == 0:
+                p_grouped[it] = work.tile([P, H * P * PACK], BF16, tag="p_grouped", bufs=1, align_bytes=64, name="p_grouped")
+            nc.gpsimd.tensor_tensor(
+                out=p_grouped[it][:, h * S : (h + 1) * S].rearrange("p (i t) -> p i t", t=PACK),
+                in0=expd[it][:].rearrange("p (t h i) -> p h i t", t=PACK, h=H)[:, h],
+                in1=inverse[it][:].rearrange("p (i t) -> p i t", t=PACK),
+                op=ALU.mult,
+            )
+
+        def quantise_probs(it):
+            cols = slice(it * A, (it + 1) * A)
+            nc.vector.quantize_mx(out=p_codes[:, cols].bitcast(FP8X4), scales=p_scales[:, cols], in_=p_grouped[it][:])
+
+        def attend(h):
+            acc = psum.tile([P, BANK], F32, tag="tp", bufs=4)
+            for it in range(ROW_TILES):
+                p_cols = slice(it * A + h * P, it * A + (h + 1) * P)
+                v_cols = slice(h * HD, (h + 1) * HD)
+                nc.tensor.matmul_mx(
+                    out=acc[:, it * HD : (it + 1) * HD],
+                    lhsT=p_codes[:, p_cols].bitcast(FP8X4),
+                    lhsT_scale=p_scales[:, p_cols],
+                    rhs=v_codes[:, v_cols].bitcast(FP8X4),
+                    rhs_scale=v_scales[:, v_cols],
+                    start=True,
+                    stop=True,
+                )
+            result = work.tile([P, BANK], F32, tag="result", bufs=4)
+            copy = nc.scalar.copy if h % 2 == 0 else nc.vector.tensor_copy
+            copy(out=result[:], in_=acc[:])
+            nc.sync.dma_start(out=out_heads[h], in_=result[:])
+
+        k_raw = load_rows(k_rows)
+        q_raw = load_rows(q_rows)
+        raws = {}
+        for s in range(AHEAD):
+            raws[s] = load_step(s)
+        transpose_heads(k_raw, kT)
+        transpose_heads(q_raw, qT)
+
+        FIRST_PROJECT = HS_STEPS + 2
+        grouped = {}
+        weights = {}
+        accs = {}
+        u = 0
+        for k in range(STEPS + 3):
+            softmax_turn = k % 4 != 3
+            if softmax_turn and 1 <= u <= UNITS:
+                exp_and_sum((u - 1) // ROW_TILES, (u - 1) % ROW_TILES)
+            if k + AHEAD < STEPS:
+                raws[k + AHEAD] = load_step(k + AHEAD)
+            if k >= FIRST_PROJECT + 2 and (k - FIRST_PROJECT) % 2 == 0:
+                h = (k - FIRST_PROJECT - 2) // 2
+                quantise_v(h, accs[h])
+            if 1 <= k <= STEPS:
+                s = k - 1
+                h = (s - HS_STEPS) // 2
+                if s >= HS_STEPS and (s - HS_STEPS) % 2 == 0:
+                    weights[h] = (
+                        work.tile([P, PASSES * HD], U32, tag="w_codes", align_bytes=64, name="w_codes"),
+                        work.tile([P, PASSES * HD], U8, tag="w_scales", align_bytes=64, name="w_scales"),
+                    )
+                w_codes, w_scales = weights.get(h, (None, None))
+                quantise_step(s, grouped[s], w_codes, w_scales)
+            if softmax_turn and u >= 2 * ROW_TILES and u % ROW_TILES == 0:
+                quantise_probs(u // ROW_TILES - 2)
+            if k < STEPS:
+                grouped[k] = transpose_step(k, raws[k])
+            if softmax_turn and u < UNITS:
+                scores_minus_max(u // ROW_TILES, u % ROW_TILES)
+            if softmax_turn and 1 <= u <= UNITS:
+                invert_sum((u - 1) // ROW_TILES, (u - 1) % ROW_TILES)
+            if softmax_turn and ROW_TILES <= u < UNITS + ROW_TILES:
+                for h in (2 * (u % ROW_TILES), 2 * (u % ROW_TILES) + 1):
+                    normalise_head(u // ROW_TILES - 1, h)
+            if FIRST_PROJECT <= k < FIRST_PROJECT + 2 * H:
+                h, second = divmod(k - FIRST_PROJECT, 2)
+                if second == 0:
+                    accs[h] = psum.tile([P, BANK], F32, tag="acc", bufs=2, name="acc")
+                w_codes, w_scales = weights[h]
+                project_groups(accs[h], 2 * second, w_codes, w_scales)
+            if softmax_turn:
+                u += 1
+        for h in range(H):
+            attend(h)

@@ -193,13 +193,13 @@ def tile_sparseattention_pb_k_kernel(tc, q_rot, k_rot, hidden_states, Wv, bv, ou
 
         p_grouped = {}
 
-        def normalise_head(it, h):
+        def normalise_heads(it, h):
             if h == 0:
                 p_grouped[it] = work.tile([P, H * P * PACK], BF16, tag="p_grouped", bufs=1, align_bytes=64, name="p_grouped")
-            nc.gpsimd.tensor_tensor(
-                out=p_grouped[it][:, h * S : (h + 1) * S].rearrange("p (i t) -> p i t", t=PACK),
-                in0=expd[it][:].rearrange("p (t h i) -> p h i t", t=PACK, h=H)[:, h],
-                in1=inverse[it][:].rearrange("p (i t) -> p i t", t=PACK),
+            nc.vector.tensor_tensor(
+                out=p_grouped[it][:, h * S : (h + 2) * S].rearrange("p (h i t) -> p h i t", h=2, t=PACK),
+                in0=expd[it][:].rearrange("p (t h i) -> p h i t", t=PACK, h=H)[:, h : h + 2],
+                in1=inverse[it][:].rearrange("p (i t) -> p i t", t=PACK).unsqueeze(1).to_broadcast([P, 2, P, PACK]),
                 op=ALU.mult,
             )
 
@@ -267,8 +267,7 @@ def tile_sparseattention_pb_k_kernel(tc, q_rot, k_rot, hidden_states, Wv, bv, ou
             if softmax_turn and 1 <= u <= UNITS:
                 invert_sum((u - 1) // ROW_TILES, (u - 1) % ROW_TILES)
             if softmax_turn and ROW_TILES <= u < UNITS + ROW_TILES:
-                for h in (2 * (u % ROW_TILES), 2 * (u % ROW_TILES) + 1):
-                    normalise_head(u // ROW_TILES - 1, h)
+                normalise_heads(u // ROW_TILES - 1, 2 * (u % ROW_TILES))
             if FIRST_PROJECT <= k < FIRST_PROJECT + 2 * H:
                 h, second = divmod(k - FIRST_PROJECT, 2)
                 if second == 0:

@@ -128,7 +128,7 @@ def tile_sparseattention_pb_k_kernel(tc, q_rot, k_rot, hidden_states, Wv, bv, ou
                         stop=(c == PASSES - 1),
                     )
 
-        def quantise_v(h, acc):
+        def add_bias(h, acc):
             v_grouped = work.tile([P, HD * PACK], BF16, tag="v_grouped", align_bytes=64)
             nc.vector.tensor_tensor(
                 out=v_grouped[:].rearrange("p (d t) -> p d t", t=PACK),
@@ -136,18 +136,20 @@ def tile_sparseattention_pb_k_kernel(tc, q_rot, k_rot, hidden_states, Wv, bv, ou
                 in1=bias[:, h * HD : (h + 1) * HD].unsqueeze(2).to_broadcast([P, HD, PACK]),
                 op=ALU.add,
             )
+            return v_grouped
+
+        def quantise_v(h, v_grouped):
             cols = slice(h * HD, (h + 1) * HD)
             nc.vector.quantize_mx(out=v_codes[:, cols].bitcast(FP8X4), scales=v_scales[:, cols], in_=v_grouped[:])
 
+        score_banks = {}
         expd = {}
-        inverse = {}
         totals = {}
+        inverse = {}
+        p_grouped = {}
 
-        def scores_minus_max(it, t):
-            if t == 0:
-                expd[it] = work.tile([P, ROW_TILES * A], F32, tag="expd", name="expd")
-                inverse[it] = work.tile([P, P * PACK], F32, tag="inverse", name="inverse")
-            banks = []
+        def scores(it, t):
+            score_banks[t] = []
             for g in range(2):
                 sc = psum.tile([P, BANK], F32, tag="sc", bufs=2, name="sc")
                 for hh in range(H // 2):
@@ -159,22 +161,29 @@ def tile_sparseattention_pb_k_kernel(tc, q_rot, k_rot, hidden_states, Wv, bv, ou
                         start=True,
                         stop=True,
                     )
-                banks.append(sc)
+                score_banks[t].append(sc)
+
+        def head_max(t):
             half_max = work.tile([P, 2 * P], F32, tag="half_max")
             for g in range(2):
                 nc.vector.tensor_reduce(
                     out=half_max[:, g * P : (g + 1) * P],
-                    in_=banks[g][:].rearrange("p (h i) -> p i h", h=H // 2),
+                    in_=score_banks[t][g][:].rearrange("p (h i) -> p i h", h=H // 2),
                     axis=AXIS.X,
                     op=ALU.max,
                 )
+            return half_max
+
+        def subtract_max(it, t, half_max):
+            if t == 0:
+                expd[it] = work.tile([P, ROW_TILES * A], F32, tag="expd", name="expd")
             top = work.tile([P, P], F32, tag="top")
             nc.vector.tensor_tensor(out=top[:], in0=half_max[:, 0:P], in1=half_max[:, P : 2 * P], op=ALU.max)
             for g in range(2):
                 first = t * A + g * BANK
                 nc.vector.tensor_tensor(
                     out=expd[it][:, first : first + BANK].rearrange("p (h i) -> p h i", h=H // 2),
-                    in0=banks[g][:].rearrange("p (h i) -> p h i", h=H // 2),
+                    in0=score_banks[t][g][:].rearrange("p (h i) -> p h i", h=H // 2),
                     in1=top[:].unsqueeze(1).to_broadcast([P, H // 2, P]),
                     op=ALU.subtract,
                 )
@@ -182,24 +191,29 @@ def tile_sparseattention_pb_k_kernel(tc, q_rot, k_rot, hidden_states, Wv, bv, ou
         def exp_and_sum(it, t):
             unit_cols = expd[it][:, t * A : (t + 1) * A]
             nc.scalar.activation(out=unit_cols, in_=unit_cols, func=ACT.Exp)
+            if t == 0:
+                totals[it] = work.tile([P, ROW_TILES * P], F32, tag="totals", name="totals")
             part = work.tile([P, 4 * P], F32, tag="part")
             nc.gpsimd.tensor_tensor(out=part[:], in0=unit_cols[:, 0 : 4 * P], in1=unit_cols[:, 4 * P : 8 * P], op=ALU.add)
             nc.gpsimd.tensor_tensor(out=part[:, 0 : 2 * P], in0=part[:, 0 : 2 * P], in1=part[:, 2 * P : 4 * P], op=ALU.add)
-            totals[t] = work.tile([P, P], F32, tag="total", name="total")
-            nc.gpsimd.tensor_tensor(out=totals[t][:], in0=part[:, 0:P], in1=part[:, P : 2 * P], op=ALU.add)
+            nc.gpsimd.tensor_tensor(out=totals[it][:, t * P : (t + 1) * P], in0=part[:, 0:P], in1=part[:, P : 2 * P], op=ALU.add)
 
-        def invert_sum(it, t):
-            nc.vector.reciprocal(out=inverse[it][:].rearrange("p (i t) -> p i t", t=PACK)[:, :, t], in_=totals[t][:])
+        def invert_sums(it):
+            log_sum = work.tile([P, ROW_TILES * P], F32, tag="log_sum")
+            nc.scalar.activation(out=log_sum[:], in_=totals[it][:], func=ACT.Ln)
+            inverse[it] = work.tile([P, P * PACK], F32, tag="inverse", name="inverse")
+            nc.scalar.activation(
+                out=inverse[it][:].rearrange("p (i t) -> p i t", t=PACK),
+                in_=log_sum[:].rearrange("p (t i) -> p i t", t=PACK),
+                func=ACT.Exp,
+                scale=-1.0,
+            )
 
-        p_grouped = {}
-
-        def normalise_heads(it, h):
-            if h == 0:
-                p_grouped[it] = work.tile([P, H * P * PACK], BF16, tag="p_grouped", bufs=1, align_bytes=64, name="p_grouped")
-            nc.vector.tensor_tensor(
-                out=p_grouped[it][:, h * S : (h + 2) * S].rearrange("p (h i t) -> p h i t", h=2, t=PACK),
-                in0=expd[it][:].rearrange("p (t h i) -> p h i t", t=PACK, h=H)[:, h : h + 2],
-                in1=inverse[it][:].rearrange("p (i t) -> p i t", t=PACK).unsqueeze(1).to_broadcast([P, 2, P, PACK]),
+        def normalise(engine, it, h, heads):
+            engine.tensor_tensor(
+                out=p_grouped[it][:, h * S : (h + heads) * S].rearrange("p (h i t) -> p h i t", h=heads, t=PACK),
+                in0=expd[it][:].rearrange("p (t h i) -> p h i t", t=PACK, h=H)[:, h : h + heads],
+                in1=inverse[it][:].rearrange("p (i t) -> p i t", t=PACK).unsqueeze(1).to_broadcast([P, heads, P, PACK]),
                 op=ALU.mult,
             )
 
@@ -234,40 +248,63 @@ def tile_sparseattention_pb_k_kernel(tc, q_rot, k_rot, hidden_states, Wv, bv, ou
         transpose_heads(k_raw, kT)
         transpose_heads(q_raw, qT)
 
+        INVERT = 1
+        MULTIPLY = (2, 3)
+        QUANTISE = 4
         FIRST_PROJECT = HS_STEPS + 2
+
+        def tile_due(turn, stage):
+            it, rest = divmod(turn - ROW_TILES - stage, ROW_TILES)
+            return it if rest == 0 and 0 <= it < ROW_TILES else None
+
         grouped = {}
         weights = {}
         accs = {}
         u = 0
         for k in range(STEPS + 3):
-            softmax_turn = k % 4 != 3
+            softmax_turn = k % 5 != 4
+            unit = divmod(u, ROW_TILES)
+            before = divmod(u - 1, ROW_TILES)
+            v_head = (k - FIRST_PROJECT - 2) // 2 if k >= FIRST_PROJECT + 2 and (k - FIRST_PROJECT) % 2 == 0 else None
             if softmax_turn and 1 <= u <= UNITS:
-                exp_and_sum((u - 1) // ROW_TILES, (u - 1) % ROW_TILES)
+                exp_and_sum(before[0], before[1])
             if k + AHEAD < STEPS:
                 raws[k + AHEAD] = load_step(k + AHEAD)
-            if k >= FIRST_PROJECT + 2 and (k - FIRST_PROJECT) % 2 == 0:
-                h = (k - FIRST_PROJECT - 2) // 2
-                quantise_v(h, accs[h])
-            if 1 <= k <= STEPS:
-                s = k - 1
-                h = (s - HS_STEPS) // 2
-                if s >= HS_STEPS and (s - HS_STEPS) % 2 == 0:
+            if softmax_turn and u < UNITS:
+                scores(unit[0], unit[1])
+            if v_head is not None:
+                v_grouped = add_bias(v_head, accs[v_head])
+            half_max = None
+            if softmax_turn and u < UNITS:
+                half_max = head_max(unit[1])
+            if v_head is not None:
+                quantise_v(v_head, v_grouped)
+            if k < STEPS:
+                grouped[k] = transpose_step(k, raws[k])
+            if softmax_turn and tile_due(u, INVERT) is not None:
+                invert_sums(tile_due(u, INVERT))
+            if softmax_turn and u < UNITS:
+                subtract_max(unit[0], unit[1], half_max)
+            for part, stage in enumerate(MULTIPLY):
+                it = tile_due(u, stage)
+                if softmax_turn and it is not None:
+                    if part == 0:
+                        p_grouped[it] = work.tile(
+                            [P, H * P * PACK], BF16, tag="p_grouped", bufs=1, align_bytes=64, name="p_grouped"
+                        )
+                    normalise(nc.vector, it, 4 * part, 3)
+                    normalise(nc.gpsimd, it, 4 * part + 3, 1)
+            if softmax_turn and tile_due(u, QUANTISE) is not None:
+                quantise_probs(tile_due(u, QUANTISE))
+            if k < STEPS:
+                h = (k - HS_STEPS) // 2
+                if k >= HS_STEPS and (k - HS_STEPS) % 2 == 0:
                     weights[h] = (
                         work.tile([P, PASSES * HD], U32, tag="w_codes", align_bytes=64, name="w_codes"),
                         work.tile([P, PASSES * HD], U8, tag="w_scales", align_bytes=64, name="w_scales"),
                     )
                 w_codes, w_scales = weights.get(h, (None, None))
-                quantise_step(s, grouped[s], w_codes, w_scales)
-            if softmax_turn and u >= 2 * ROW_TILES and u % ROW_TILES == 0:
-                quantise_probs(u // ROW_TILES - 2)
-            if k < STEPS:
-                grouped[k] = transpose_step(k, raws[k])
-            if softmax_turn and u < UNITS:
-                scores_minus_max(u // ROW_TILES, u % ROW_TILES)
-            if softmax_turn and 1 <= u <= UNITS:
-                invert_sum((u - 1) // ROW_TILES, (u - 1) % ROW_TILES)
-            if softmax_turn and ROW_TILES <= u < UNITS + ROW_TILES:
-                normalise_heads(u // ROW_TILES - 1, 2 * (u % ROW_TILES))
+                quantise_step(k, grouped[k], w_codes, w_scales)
             if FIRST_PROJECT <= k < FIRST_PROJECT + 2 * H:
                 h, second = divmod(k - FIRST_PROJECT, 2)
                 if second == 0:

@@ -36,7 +36,6 @@ FLOPS = 2 * S * A * D + 2 * 2 * H * S * S * HD
 def tile_sparseattention_pb_k_kernel(tc, q_rot, k_rot, hidden_states, Wv, bv, out):
     nc = tc.nc
     with ExitStack() as ctx:
-        ctx.enter_context(tc.manual_schedule())
         keep = ctx.enter_context(tc.tile_pool(name="keep", bufs=1))
         work = ctx.enter_context(tc.tile_pool(name="work", bufs=2))
         psum = ctx.enter_context(tc.psum_pool(name="psum", bufs=2))

@@ -23,6 +23,7 @@ HD = A // H
 ROW_TILES = S // P
 PASSES = D // K_PASS
 BANK = 512
+HALF = BANK // H
 RAW = 4096
 HS_STEPS = S * D // (P * RAW)
 WV_STEPS = A * D // (P * RAW)
@@ -36,6 +37,7 @@ FLOPS = 2 * S * A * D + 2 * 2 * H * S * S * HD
 def tile_sparseattention_pb_k_kernel(tc, q_rot, k_rot, hidden_states, Wv, bv, out):
     nc = tc.nc
     with ExitStack() as ctx:
+        ctx.enter_context(tc.manual_schedule())
         keep = ctx.enter_context(tc.tile_pool(name="keep", bufs=1))
         work = ctx.enter_context(tc.tile_pool(name="work", bufs=2))
         psum = ctx.enter_context(tc.psum_pool(name="psum", bufs=2))
@@ -148,42 +150,38 @@ def tile_sparseattention_pb_k_kernel(tc, q_rot, k_rot, hidden_states, Wv, bv, ou
         p_grouped = {}
 
         def scores(it, t):
-            score_banks[t] = []
-            for g in range(2):
-                sc = psum.tile([P, BANK], F32, tag="sc", bufs=2, name="sc")
-                for hh in range(H // 2):
-                    h = g * (H // 2) + hh
+            score_banks[t] = [psum.tile([P, BANK], F32, tag="sc", bufs=2, name="sc") for g in range(2)]
+            for h in range(H):
+                for g in range(2):
+                    first = h * S + it * P + g * HALF
                     nc.tensor.matmul(
-                        out=sc[:, hh * P : (hh + 1) * P],
+                        out=score_banks[t][g][:, h * HALF : (h + 1) * HALF],
                         lhsT=kT[:, h * S + t * P : h * S + (t + 1) * P],
-                        rhs=qT[:, h * S + it * P : h * S + (it + 1) * P],
+                        rhs=qT[:, first : first + HALF],
                         start=True,
                         stop=True,
                     )
-                score_banks[t].append(sc)
 
         def head_max(t):
-            half_max = work.tile([P, 2 * P], F32, tag="half_max")
+            top = work.tile([P, P], F32, tag="top")
             for g in range(2):
                 nc.vector.tensor_reduce(
-                    out=half_max[:, g * P : (g + 1) * P],
-                    in_=score_banks[t][g][:].rearrange("p (h i) -> p i h", h=H // 2),
+                    out=top[:, g * HALF : (g + 1) * HALF],
+                    in_=score_banks[t][g][:].rearrange("p (h i) -> p i h", h=H),
                     axis=AXIS.X,
                     op=ALU.max,
                 )
-            return half_max
+            return top
 
-        def subtract_max(it, t, half_max):
+        def subtract_max(it, t, top):
             if t == 0:
                 expd[it] = work.tile([P, ROW_TILES * A], F32, tag="expd", name="expd")
-            top = work.tile([P, P], F32, tag="top")
-            nc.vector.tensor_tensor(out=top[:], in0=half_max[:, 0:P], in1=half_max[:, P : 2 * P], op=ALU.max)
+            unit_cols = expd[it][:, t * A : (t + 1) * A].rearrange("p (h i) -> p h i", h=H)
             for g in range(2):
-                first = t * A + g * BANK
                 nc.vector.tensor_tensor(
-                    out=expd[it][:, first : first + BANK].rearrange("p (h i) -> p h i", h=H // 2),
-                    in0=score_banks[t][g][:].rearrange("p (h i) -> p h i", h=H // 2),
-                    in1=top[:].unsqueeze(1).to_broadcast([P, H // 2, P]),
+                    out=unit_cols[:, :, g * HALF : (g + 1) * HALF],
+                    in0=score_banks[t][g][:].rearrange("p (h i) -> p h i", h=H),
+                    in1=top[:, g * HALF : (g + 1) * HALF].unsqueeze(1).to_broadcast([P, H, HALF]),
                     op=ALU.subtract,
                 )
 
@@ -208,8 +206,8 @@ def tile_sparseattention_pb_k_kernel(tc, q_rot, k_rot, hidden_states, Wv, bv, ou
                 scale=-1.0,
             )
 
-        def normalise(engine, it, h, heads):
-            engine.tensor_tensor(
+        def normalise(it, h, heads):
+            nc.vector.tensor_tensor(
                 out=p_grouped[it][:, h * S : (h + heads) * S].rearrange("p (h i t) -> p h i t", h=heads, t=PACK),
                 in0=expd[it][:].rearrange("p (t h i) -> p h i t", t=PACK, h=H)[:, h : h + heads],
                 in1=inverse[it][:].rearrange("p (i t) -> p i t", t=PACK).unsqueeze(1).to_broadcast([P, heads, P, PACK]),
@@ -273,9 +271,9 @@ def tile_sparseattention_pb_k_kernel(tc, q_rot, k_rot, hidden_states, Wv, bv, ou
                 scores(unit[0], unit[1])
             if v_head is not None:
                 v_grouped = add_bias(v_head, accs[v_head])
-            half_max = None
+            top = None
             if softmax_turn and u < UNITS:
-                half_max = head_max(unit[1])
+                top = head_max(unit[1])
             if v_head is not None:
                 quantise_v(v_head, v_grouped)
             if k < STEPS:
@@ -283,7 +281,7 @@ def tile_sparseattention_pb_k_kernel(tc, q_rot, k_rot, hidden_states, Wv, bv, ou
             if softmax_turn and tile_due(u, INVERT) is not None:
                 invert_sums(tile_due(u, INVERT))
             if softmax_turn and u < UNITS:
-                subtract_max(unit[0], unit[1], half_max)
+                subtract_max(unit[0], unit[1], top)
             for part, stage in enumerate(MULTIPLY):
                 it = tile_due(u, stage)
                 if softmax_turn and it is not None:
@@ -291,8 +289,7 @@ def tile_sparseattention_pb_k_kernel(tc, q_rot, k_rot, hidden_states, Wv, bv, ou
                         p_grouped[it] = work.tile(
                             [P, H * P * PACK], BF16, tag="p_grouped", bufs=1, align_bytes=64, name="p_grouped"
                         )
-                    normalise(nc.vector, it, 4 * part, 3)
-                    normalise(nc.gpsimd, it, 4 * part + 3, 1)
+                    normalise(it, 4 * part, 4)
             if softmax_turn and tile_due(u, QUANTISE) is not None:
                 quantise_probs(tile_due(u, QUANTISE))
             if k < STEPS:

@@ -74,16 +74,15 @@ def tile_sparseattention_pb_k_kernel(tc, q_rot, k_rot, hidden_states, Wv, bv, ou
             h, half = divmod(s - HS_STEPS, 2)
             return load_rows(Wv[h * HD : (h + 1) * HD, half * RAW : (half + 1) * RAW].unsqueeze(1))
 
-        def transpose_heads(raw, dst):
-            for pair in range(H // 2):
-                bank = psum.tile([P, 2 * BANK], BF16, tag="tp", bufs=4)
-                for hh in range(2):
-                    for t in range(ROW_TILES):
-                        col = t * A + (2 * pair + hh) * HD
-                        slot = (hh * ROW_TILES + t) * P
-                        nc.tensor.transpose(bank[:, slot : slot + P], raw[:, col : col + HD], ident_bf16[:])
-                copy = nc.scalar.copy if pair % 2 == 0 else nc.vector.tensor_copy
-                copy(out=dst[:, pair * 2 * BANK : (pair + 1) * 2 * BANK], in_=bank[:])
+        def transpose_row_tile(raw, dst, t, copy):
+            bank = psum.tile([P, 2 * BANK], BF16, tag="tp", bufs=4)
+            for h in range(H):
+                col = t * A + h * HD
+                nc.tensor.transpose(bank[:, h * P : (h + 1) * P], raw[:, col : col + HD], ident_bf16[:])
+            copy(
+                out=dst[:].rearrange("p (h t r) -> p h t r", h=H, t=ROW_TILES)[:, :, t, :],
+                in_=bank[:].rearrange("p (h r) -> p h r", h=H),
+            )
 
         def transpose_step(s, raw):
             words = raw[:].bitcast(F32)
@@ -237,13 +236,16 @@ def tile_sparseattention_pb_k_kernel(tc, q_rot, k_rot, hidden_states, Wv, bv, ou
             copy(out=result[:], in_=acc[:])
             nc.sync.dma_start(out=out_heads[h], in_=result[:])
 
-        k_raw = load_rows(k_rows)
-        q_raw = load_rows(q_rows)
+        k_raw = work.tile([P, RAW], BF16, tag="raw", bufs=AHEAD + 2)
+        q_raw = work.tile([P, RAW], BF16, tag="raw", bufs=AHEAD + 2)
+        for t in range(ROW_TILES):
+            nc.sync.dma_start(out=k_raw[:, t * A : (t + 1) * A], in_=k_rows[:, t, :])
+            nc.sync.dma_start(out=q_raw[:, t * A : (t + 1) * A], in_=q_rows[:, t, :])
         raws = {}
         for s in range(AHEAD):
             raws[s] = load_step(s)
-        transpose_heads(k_raw, kT)
-        transpose_heads(q_raw, qT)
+        transpose_row_tile(k_raw, kT, 0, nc.scalar.copy)
+        transpose_row_tile(q_raw, qT, 0, nc.vector.tensor_copy)
 
         INVERT = 1
         MULTIPLY = (2, 3)
@@ -269,6 +271,10 @@ def tile_sparseattention_pb_k_kernel(tc, q_rot, k_rot, hidden_states, Wv, bv, ou
                 raws[k + AHEAD] = load_step(k + AHEAD)
             if softmax_turn and u < UNITS:
                 scores(unit[0], unit[1])
+            if k == 0:
+                for t in range(1, ROW_TILES):
+                    transpose_row_tile(k_raw, kT, t, nc.scalar.copy)
+                    transpose_row_tile(q_raw, qT, t, nc.scalar.copy)
             if v_head is not None:
                 v_grouped = add_bias(v_head, accs[v_head])
             top = None

@@ -47,12 +47,11 @@ def tile_sparseattention_pb_k_kernel(tc, q_rot, k_rot, hidden_states, Wv, bv, ou
         hs_rows = hidden_states.flatten_outer_dims().rearrange("(p t) k -> p t k", t=ROW_TILES)
         out_heads = out.flatten_outer_dims().rearrange("(h a) (b x) -> h (a b) x", h=H, b=2)
 
-        ident_f32 = keep.tile([P, P], F32)
-        make_identity(nc, ident_f32[:])
         ident_bf16 = keep.tile([P, P], BF16)
         make_identity(nc, ident_bf16[:])
+        ident_f32 = keep.tile([P, P], F32)
+        make_identity(nc, ident_f32[:])
         bias = keep.tile([P, A], BF16)
-        nc.scalar.dma_start(out=bias[:], in_=bv.partition_broadcast(P))
 
         qT = keep.tile([P, A * ROW_TILES], BF16)
         kT = keep.tile([P, A * ROW_TILES], BF16)
@@ -244,6 +243,7 @@ def tile_sparseattention_pb_k_kernel(tc, q_rot, k_rot, hidden_states, Wv, bv, ou
         raws = {}
         for s in range(AHEAD):
             raws[s] = load_step(s)
+        nc.sync.dma_start(out=bias[:], in_=bv.partition_broadcast(P))
         transpose_row_tile(k_raw, kT, 0, nc.scalar.copy)
         transpose_row_tile(q_raw, qT, 0, nc.vector.tensor_copy)
 

@@ -25,11 +25,14 @@ PASSES = D // K_PASS
 BANK = 512
 HALF = BANK // H
 RAW = 4096
+GROUPED = RAW // 2
 HS_STEPS = S * D // (P * RAW)
 WV_STEPS = A * D // (P * RAW)
 STEPS = HS_STEPS + WV_STEPS
 UNITS = ROW_TILES * ROW_TILES
-AHEAD = 3
+AHEAD = 2
+BATCH = 2
+QUAD = 4
 
 FLOPS = 2 * S * A * D + 2 * 2 * H * S * S * HD
 
@@ -53,8 +56,7 @@ def tile_sparseattention_pb_k_kernel(tc, q_rot, k_rot, hidden_states, Wv, bv, ou
         make_identity(nc, ident_f32[:])
         bias = keep.tile([P, A], BF16)
 
-        qT = keep.tile([P, A * ROW_TILES], BF16)
-        kT = keep.tile([P, A * ROW_TILES], BF16)
+        kT = keep.tile([P, ROW_TILES * A], BF16)
         hs_codes = keep.tile([P, PASSES * S], U32, align_bytes=64)
         hs_scales = keep.tile([P, PASSES * S], U8, align_bytes=64)
         p_codes = keep.tile([P, H * S], U32, align_bytes=64)
@@ -62,32 +64,40 @@ def tile_sparseattention_pb_k_kernel(tc, q_rot, k_rot, hidden_states, Wv, bv, ou
         v_codes = keep.tile([P, A], U32, align_bytes=64)
         v_scales = keep.tile([P, A], U8, align_bytes=64)
 
-        def load_rows(view):
-            raw = work.tile([P, RAW], BF16, tag="raw", bufs=AHEAD + 2)
-            nc.sync.dma_start(out=raw[:].rearrange("p (t c) -> p t c", t=view.shape[1]), in_=view)
+        def load_step(s, pieces=1):
+            raw = work.tile([P, RAW], BF16, tag="raw", bufs=AHEAD + 1)
+            if s < HS_STEPS:
+                width = RAW // ROW_TILES
+                view = hs_rows[:, :, s * width : (s + 1) * width]
+                dst = raw[:].rearrange("p (t c) -> p t c", t=ROW_TILES)
+                piece = width // pieces
+                for i in range(pieces):
+                    cols = slice(i * piece, (i + 1) * piece)
+                    nc.sync.dma_start(out=dst[:, :, cols], in_=view[:, :, cols])
+            else:
+                h, half = divmod(s - HS_STEPS, 2)
+                nc.sync.dma_start(out=raw[:], in_=Wv[h * HD : (h + 1) * HD, half * RAW : (half + 1) * RAW])
             return raw
 
-        def load_step(s):
-            if s < HS_STEPS:
-                return load_rows(hs_rows[:, :, s * (RAW // ROW_TILES) : (s + 1) * (RAW // ROW_TILES)])
-            h, half = divmod(s - HS_STEPS, 2)
-            return load_rows(Wv[h * HD : (h + 1) * HD, half * RAW : (half + 1) * RAW].unsqueeze(1))
+        def load_rows(rows, t):
+            raw = work.tile([P, A], BF16, tag="qk_raw", bufs=3)
+            nc.sync.dma_start(out=raw[:], in_=rows[:, t, :])
+            return raw
 
-        def transpose_row_tile(raw, dst, t, copy):
-            bank = psum.tile([P, 2 * BANK], BF16, tag="tp", bufs=4)
+        def transpose_rows(raw, dst, copy):
+            bank = psum.tile([P, A], BF16, tag="tp", bufs=4)
             for h in range(H):
-                col = t * A + h * HD
-                nc.tensor.transpose(bank[:, h * P : (h + 1) * P], raw[:, col : col + HD], ident_bf16[:])
-            copy(
-                out=dst[:].rearrange("p (h t r) -> p h t r", h=H, t=ROW_TILES)[:, :, t, :],
-                in_=bank[:].rearrange("p (h r) -> p h r", h=H),
-            )
+                nc.tensor.transpose(bank[:, h * P : (h + 1) * P], raw[:, h * HD : (h + 1) * HD], ident_bf16[:])
+            copy(out=dst, in_=bank[:])
 
         def transpose_step(s, raw):
             words = raw[:].bitcast(F32)
-            grouped = work.tile([P, RAW], BF16, tag="grouped", bufs=2, align_bytes=64)
-            grouped_words = grouped[:].bitcast(F32)
+            halves = []
             for b in range(RAW // 2 // BANK):
+                if b % 2 == 0:
+                    grouped = work.tile([P, GROUPED], BF16, tag="grouped", bufs=3, align_bytes=64)
+                    halves.append(grouped)
+                grouped_words = halves[-1][:].bitcast(F32)
                 bank = psum.tile([P, BANK], F32, tag="tp", bufs=4)
                 for a in range(2):
                     for u in range(2):
@@ -98,34 +108,36 @@ def tile_sparseattention_pb_k_kernel(tc, q_rot, k_rot, hidden_states, Wv, bv, ou
                         slot = (2 * a + u) * P
                         nc.tensor.transpose(bank[:, slot : slot + P], words[:, blk * P : (blk + 1) * P], ident_f32[:])
                 nc.scalar.copy(
-                    out=grouped_words[:, b * BANK : (b + 1) * BANK].rearrange("p (a r u) -> p a r u", a=2, u=2),
+                    out=grouped_words[:, (b % 2) * BANK : (b % 2 + 1) * BANK].rearrange("p (a r u) -> p a r u", a=2, u=2),
                     in_=bank[:].rearrange("p (a u r) -> p a r u", a=2, u=2),
                 )
-            return grouped
+            return halves
 
-        def quantise_step(s, grouped, w_codes, w_scales):
-            if s < HS_STEPS:
-                cols = slice(s * (RAW // PACK), (s + 1) * (RAW // PACK))
-                nc.vector.quantize_mx(out=hs_codes[:, cols].bitcast(FP8X4), scales=hs_scales[:, cols], in_=grouped[:])
-            else:
-                half = (s - HS_STEPS) % 2
-                cols = slice(half * (RAW // PACK), (half + 1) * (RAW // PACK))
-                nc.vector.quantize_mx(out=w_codes[:, cols].bitcast(FP8X4), scales=w_scales[:, cols], in_=grouped[:])
+        def quantise_step(s, halves, w_codes, w_scales):
+            for i, grouped in enumerate(halves):
+                width = GROUPED // PACK
+                if s < HS_STEPS:
+                    first = s * (RAW // PACK) + i * width
+                    codes, scales = hs_codes, hs_scales
+                else:
+                    first = ((s - HS_STEPS) % 2) * (RAW // PACK) + i * width
+                    codes, scales = w_codes, w_scales
+                cols = slice(first, first + width)
+                nc.vector.quantize_mx(out=codes[:, cols].bitcast(FP8X4), scales=scales[:, cols], in_=grouped[:])
 
-        def project_groups(acc, first_t, w_codes, w_scales):
-            for t in range(first_t, first_t + 2):
-                for c in range(PASSES):
-                    hs_cols = slice(c * S + t * P, c * S + (t + 1) * P)
-                    w_cols = slice(c * HD, (c + 1) * HD)
-                    nc.tensor.matmul_mx(
-                        out=acc[:, t * HD : (t + 1) * HD],
-                        lhsT=hs_codes[:, hs_cols].bitcast(FP8X4),
-                        lhsT_scale=hs_scales[:, hs_cols],
-                        rhs=w_codes[:, w_cols].bitcast(FP8X4),
-                        rhs_scale=w_scales[:, w_cols],
-                        start=(c == 0),
-                        stop=(c == PASSES - 1),
-                    )
+        def project(acc, t, w_codes, w_scales, passes):
+            for c in passes:
+                hs_cols = slice(c * S + t * P, c * S + (t + 1) * P)
+                w_cols = slice(c * HD, (c + 1) * HD)
+                nc.tensor.matmul_mx(
+                    out=acc[:, t * HD : (t + 1) * HD],
+                    lhsT=hs_codes[:, hs_cols].bitcast(FP8X4),
+                    lhsT_scale=hs_scales[:, hs_cols],
+                    rhs=w_codes[:, w_cols].bitcast(FP8X4),
+                    rhs_scale=w_scales[:, w_cols],
+                    start=(c == passes[0]),
+                    stop=(c == passes[-1]),
+                )
 
         def add_bias(h, acc):
             v_grouped = work.tile([P, HD * PACK], BF16, tag="v_grouped", align_bytes=64)
@@ -137,87 +149,118 @@ def tile_sparseattention_pb_k_kernel(tc, q_rot, k_rot, hidden_states, Wv, bv, ou
             )
             return v_grouped
 
+        def bias_and_part(h, acc):
+            part = work.tile([P, BANK], F32, tag="result", bufs=2)
+            nc.vector.tensor_tensor(
+                out=part[:].rearrange("p (t d) -> p t d", t=PACK),
+                in0=acc[:].rearrange("p (t d) -> p t d", t=PACK),
+                in1=bias[:, h * HD : (h + 1) * HD].unsqueeze(1).to_broadcast([P, PACK, HD]),
+                op=ALU.add,
+            )
+            return part
+
+        def add_part(acc, part):
+            v_grouped = work.tile([P, HD * PACK], BF16, tag="v_grouped", align_bytes=64)
+            nc.vector.tensor_tensor(
+                out=v_grouped[:].rearrange("p (d t) -> p d t", t=PACK),
+                in0=acc[:].rearrange("p (t d) -> p d t", t=PACK),
+                in1=part[:].rearrange("p (t d) -> p d t", t=PACK),
+                op=ALU.add,
+            )
+            return v_grouped
+
         def quantise_v(h, v_grouped):
             cols = slice(h * HD, (h + 1) * HD)
             nc.vector.quantize_mx(out=v_codes[:, cols].bitcast(FP8X4), scales=v_scales[:, cols], in_=v_grouped[:])
 
         score_banks = {}
+        qT = {}
         expd = {}
         totals = {}
         inverse = {}
-        p_grouped = {}
 
-        def scores(it, t):
-            score_banks[t] = [psum.tile([P, BANK], F32, tag="sc", bufs=2, name="sc") for g in range(2)]
+        def scores(unit):
+            it, t = divmod(unit, ROW_TILES)
+            score_banks[unit] = [psum.tile([P, BANK], F32, tag="sc", bufs=2, name="sc") for g in range(2)]
             for h in range(H):
                 for g in range(2):
-                    first = h * S + it * P + g * HALF
+                    first = h * P + g * HALF
                     nc.tensor.matmul(
-                        out=score_banks[t][g][:, h * HALF : (h + 1) * HALF],
-                        lhsT=kT[:, h * S + t * P : h * S + (t + 1) * P],
-                        rhs=qT[:, first : first + HALF],
+                        out=score_banks[unit][g][:, h * HALF : (h + 1) * HALF],
+                        lhsT=kT[:, t * A + h * HD : t * A + (h + 1) * HD],
+                        rhs=qT[it][:, first : first + HALF],
                         start=True,
                         stop=True,
                     )
 
-        def head_max(t):
+        def subtract_max(unit):
+            it, t = divmod(unit, ROW_TILES)
+            banks = score_banks[unit]
             top = work.tile([P, P], F32, tag="top")
             for g in range(2):
                 nc.vector.tensor_reduce(
                     out=top[:, g * HALF : (g + 1) * HALF],
-                    in_=score_banks[t][g][:].rearrange("p (h i) -> p i h", h=H),
+                    in_=banks[g][:].rearrange("p (h i) -> p i h", h=H),
                     axis=AXIS.X,
                     op=ALU.max,
                 )
-            return top
-
-        def subtract_max(it, t, top):
             if t == 0:
-                expd[it] = work.tile([P, ROW_TILES * A], F32, tag="expd", name="expd")
+                expd[it] = work.tile([P, ROW_TILES * A], F32, tag="expd", bufs=4, name="expd")
             unit_cols = expd[it][:, t * A : (t + 1) * A].rearrange("p (h i) -> p h i", h=H)
             for g in range(2):
                 nc.vector.tensor_tensor(
                     out=unit_cols[:, :, g * HALF : (g + 1) * HALF],
-                    in0=score_banks[t][g][:].rearrange("p (h i) -> p h i", h=H),
+                    in0=banks[g][:].rearrange("p (h i) -> p h i", h=H),
                     in1=top[:, g * HALF : (g + 1) * HALF].unsqueeze(1).to_broadcast([P, H, HALF]),
                     op=ALU.subtract,
                 )
 
-        def exp_and_sum(it, t):
+        def exp_and_sum(unit):
+            it, t = divmod(unit, ROW_TILES)
+            batch, member = divmod(it, BATCH)
             unit_cols = expd[it][:, t * A : (t + 1) * A]
             nc.scalar.activation(out=unit_cols, in_=unit_cols, func=ACT.Exp)
-            if t == 0:
-                totals[it] = work.tile([P, ROW_TILES * P], F32, tag="totals", name="totals")
-            part = work.tile([P, 4 * P], F32, tag="part")
+            if member == 0 and t == 0:
+                totals[batch] = work.tile([P, BATCH * ROW_TILES * P], F32, tag="totals", name="totals")
+            part = work.tile([P, 4 * P], F32, tag="part", bufs=1)
+            first = (member * ROW_TILES + t) * P
             nc.gpsimd.tensor_tensor(out=part[:], in0=unit_cols[:, 0 : 4 * P], in1=unit_cols[:, 4 * P : 8 * P], op=ALU.add)
             nc.gpsimd.tensor_tensor(out=part[:, 0 : 2 * P], in0=part[:, 0 : 2 * P], in1=part[:, 2 * P : 4 * P], op=ALU.add)
-            nc.gpsimd.tensor_tensor(out=totals[it][:, t * P : (t + 1) * P], in0=part[:, 0:P], in1=part[:, P : 2 * P], op=ALU.add)
+            nc.gpsimd.tensor_tensor(out=totals[batch][:, first : first + P], in0=part[:, 0:P], in1=part[:, P : 2 * P], op=ALU.add)
 
-        def invert_sums(it):
-            log_sum = work.tile([P, ROW_TILES * P], F32, tag="log_sum")
-            nc.scalar.activation(out=log_sum[:], in_=totals[it][:], func=ACT.Ln)
-            inverse[it] = work.tile([P, P * PACK], F32, tag="inverse", name="inverse")
-            nc.scalar.activation(
-                out=inverse[it][:].rearrange("p (i t) -> p i t", t=PACK),
-                in_=log_sum[:].rearrange("p (t i) -> p i t", t=PACK),
-                func=ACT.Exp,
-                scale=-1.0,
-            )
+        def log_sums(batch):
+            nc.scalar.activation(out=totals[batch][:], in_=totals[batch][:], func=ACT.Ln)
 
-        def normalise(it, h, heads):
+        def invert_sums(batch):
+            inverse[batch] = work.tile([P, BATCH * P * PACK], F32, tag="inverse", name="inverse")
+            for member in range(BATCH):
+                cols = slice(member * S, (member + 1) * S)
+                nc.scalar.activation(
+                    out=inverse[batch][:, cols].rearrange("p (i t) -> p i t", t=PACK),
+                    in_=totals[batch][:, cols].rearrange("p (t i) -> p i t", t=PACK),
+                    func=ACT.Exp,
+                    scale=-1.0,
+                )
+
+        def normalise(it, h, heads, p_grouped, at):
+            batch, member = divmod(it, BATCH)
             nc.vector.tensor_tensor(
-                out=p_grouped[it][:, h * S : (h + heads) * S].rearrange("p (h i t) -> p h i t", h=heads, t=PACK),
+                out=p_grouped[:, at * S : (at + heads) * S].rearrange("p (h i t) -> p h i t", h=heads, t=PACK),
                 in0=expd[it][:].rearrange("p (t h i) -> p h i t", t=PACK, h=H)[:, h : h + heads],
-                in1=inverse[it][:].rearrange("p (i t) -> p i t", t=PACK).unsqueeze(1).to_broadcast([P, heads, P, PACK]),
+                in1=inverse[batch][:, member * S : (member + 1) * S]
+                .rearrange("p (i t) -> p i t", t=PACK)
+                .unsqueeze(1)
+                .to_broadcast([P, heads, P, PACK]),
                 op=ALU.mult,
             )
 
-        def quantise_probs(it):
-            cols = slice(it * A, (it + 1) * A)
-            nc.vector.quantize_mx(out=p_codes[:, cols].bitcast(FP8X4), scales=p_scales[:, cols], in_=p_grouped[it][:])
+        def quantise_probs(it, quad, p_grouped):
+            first = it * A + quad * QUAD * P
+            cols = slice(first, first + QUAD * P)
+            nc.vector.quantize_mx(out=p_codes[:, cols].bitcast(FP8X4), scales=p_scales[:, cols], in_=p_grouped[:])
 
         def attend(h):
-            acc = psum.tile([P, BANK], F32, tag="tp", bufs=4)
+            acc = psum.tile([P, BANK], F32, tag="sc", bufs=2, name="attended")
             for it in range(ROW_TILES):
                 p_cols = slice(it * A + h * P, it * A + (h + 1) * P)
                 v_cols = slice(h * HD, (h + 1) * HD)
@@ -230,90 +273,125 @@ def tile_sparseattention_pb_k_kernel(tc, q_rot, k_rot, hidden_states, Wv, bv, ou
                     start=True,
                     stop=True,
                 )
-            result = work.tile([P, BANK], F32, tag="result", bufs=4)
-            copy = nc.scalar.copy if h % 2 == 0 else nc.vector.tensor_copy
-            copy(out=result[:], in_=acc[:])
+            result = work.tile([P, BANK], F32, tag="result", bufs=2)
+            nc.scalar.copy(out=result[:], in_=acc[:])
             nc.sync.dma_start(out=out_heads[h], in_=result[:])
 
-        k_raw = work.tile([P, RAW], BF16, tag="raw", bufs=AHEAD + 2)
-        q_raw = work.tile([P, RAW], BF16, tag="raw", bufs=AHEAD + 2)
-        for t in range(ROW_TILES):
-            nc.sync.dma_start(out=k_raw[:, t * A : (t + 1) * A], in_=k_rows[:, t, :])
-            nc.sync.dma_start(out=q_raw[:, t * A : (t + 1) * A], in_=q_rows[:, t, :])
         raws = {}
-        for s in range(AHEAD):
-            raws[s] = load_step(s)
-        nc.sync.dma_start(out=bias[:], in_=bv.partition_broadcast(P))
-        transpose_row_tile(k_raw, kT, 0, nc.scalar.copy)
-        transpose_row_tile(q_raw, qT, 0, nc.vector.tensor_copy)
+        k_raw = {}
+        q_raw = {}
+        k_raw[0] = load_rows(k_rows, 0)
+        q_raw[0] = load_rows(q_rows, 0)
+        raws[0] = load_step(0, pieces=2)
+        k_raw[1] = load_rows(k_rows, 1)
+        raws[1] = load_step(1)
+        transpose_rows(k_raw[0], kT[:, 0:A], nc.scalar.copy)
+        qT[0] = work.tile([P, A], BF16, tag="qT", name="qT")
+        transpose_rows(q_raw[0], qT[0][:], nc.vector.tensor_copy)
+        scores(0)
+        for t in range(2, ROW_TILES):
+            k_raw[t] = load_rows(k_rows, t)
 
-        INVERT = 1
-        MULTIPLY = (2, 3)
-        QUANTISE = 4
         FIRST_PROJECT = HS_STEPS + 2
+        LAST = H - 1
+        HALVES = (range(PASSES // 2), range(PASSES // 2, PASSES))
+        units_of_batch = BATCH * ROW_TILES
 
-        def tile_due(turn, stage):
-            it, rest = divmod(turn - ROW_TILES - stage, ROW_TILES)
-            return it if rest == 0 and 0 <= it < ROW_TILES else None
-
+        loaded = {}
         grouped = {}
         weights = {}
         accs = {}
-        u = 0
+        normal_queue = []
+        half_done = {}
+        to_quantise = []
+        probs_ready = {}
+        v_ready = set()
+        attended = 0
         for k in range(STEPS + 3):
-            softmax_turn = k % 5 != 4
-            unit = divmod(u, ROW_TILES)
-            before = divmod(u - 1, ROW_TILES)
-            v_head = (k - FIRST_PROJECT - 2) // 2 if k >= FIRST_PROJECT + 2 and (k - FIRST_PROJECT) % 2 == 0 else None
-            if softmax_turn and 1 <= u <= UNITS:
-                exp_and_sum(before[0], before[1])
+            if k % ROW_TILES == 1 and k // ROW_TILES + 1 < ROW_TILES:
+                q_raw[k // ROW_TILES + 1] = load_rows(q_rows, k // ROW_TILES + 1)
             if k + AHEAD < STEPS:
                 raws[k + AHEAD] = load_step(k + AHEAD)
-            if softmax_turn and u < UNITS:
-                scores(unit[0], unit[1])
-            if k == 0:
-                for t in range(1, ROW_TILES):
-                    transpose_row_tile(k_raw, kT, t, nc.scalar.copy)
-                    transpose_row_tile(q_raw, qT, t, nc.scalar.copy)
-            if v_head is not None:
-                v_grouped = add_bias(v_head, accs[v_head])
-            top = None
-            if softmax_turn and u < UNITS:
-                top = head_max(unit[1])
-            if v_head is not None:
-                quantise_v(v_head, v_grouped)
+            if k == ROW_TILES:
+                nc.sync.dma_start(out=bias[:], in_=bv.partition_broadcast(P))
+
+            if k < UNITS:
+                subtract_max(k)
             if k < STEPS:
                 grouped[k] = transpose_step(k, raws[k])
-            if softmax_turn and tile_due(u, INVERT) is not None:
-                invert_sums(tile_due(u, INVERT))
-            if softmax_turn and u < UNITS:
-                subtract_max(unit[0], unit[1], top)
-            for part, stage in enumerate(MULTIPLY):
-                it = tile_due(u, stage)
-                if softmax_turn and it is not None:
-                    if part == 0:
-                        p_grouped[it] = work.tile(
-                            [P, H * P * PACK], BF16, tag="p_grouped", bufs=1, align_bytes=64, name="p_grouped"
-                        )
-                    normalise(it, 4 * part, 4)
-            if softmax_turn and tile_due(u, QUANTISE) is not None:
-                quantise_probs(tile_due(u, QUANTISE))
+            if k + 1 < ROW_TILES:
+                transpose_rows(k_raw[k + 1], kT[:, (k + 1) * A : (k + 2) * A], nc.scalar.copy)
+            if (k + 1) % ROW_TILES == 0 and k + 1 < UNITS:
+                it = (k + 1) // ROW_TILES
+                qT[it] = work.tile([P, A], BF16, tag="qT", name="qT")
+                transpose_rows(q_raw[it], qT[it][:], nc.scalar.copy)
+
+            head, second = divmod(k - FIRST_PROJECT, 2)
+            projecting = 0 <= head < LAST
+            if projecting:
+                if second == 0:
+                    accs[head] = psum.tile([P, BANK], F32, tag="acc", bufs=2, name="acc")
+                project(accs[head], 2 * second, *weights[head], range(PASSES))
+            if k + 1 < UNITS:
+                scores(k + 1)
+            if projecting:
+                project(accs[head], 2 * second + 1, *weights[head], range(PASSES))
+            if k == STEPS - 1:
+                accs[LAST] = psum.tile([P, BANK], F32, tag="acc", bufs=2, name="acc")
+                for t in range(ROW_TILES):
+                    project(accs[LAST], t, *weights[LAST], HALVES[0])
+
+            if k < UNITS:
+                exp_and_sum(k)
+            for batch in range(ROW_TILES // BATCH):
+                if k == (batch + 1) * units_of_batch:
+                    log_sums(batch)
+                if k == (batch + 1) * units_of_batch + 1:
+                    invert_sums(batch)
+                    for quad in range(H // QUAD):
+                        for it in range(batch * BATCH, (batch + 1) * BATCH):
+                            for h in range(quad * QUAD, (quad + 1) * QUAD, 2):
+                                normal_queue.append((it, h, k + 1))
+
+            for it, quad, p_grouped in to_quantise:
+                quantise_probs(it, quad, p_grouped)
+                probs_ready[quad] = probs_ready.get(quad, 0) + 1
+            to_quantise = []
+            v_head = (k - FIRST_PROJECT - 2) // 2 if k >= FIRST_PROJECT + 2 and (k - FIRST_PROJECT) % 2 == 0 else None
+            if v_head is not None and v_head >= LAST:
+                v_head = None
+            room = 2 if k >= UNITS else (1 if v_head is None else 0)
+            while room > 0 and normal_queue and normal_queue[0][2] <= k:
+                it, h, ready = normal_queue.pop(0)
+                quad, at = divmod(h, QUAD)
+                if at == 0:
+                    half_done[it] = work.tile([P, QUAD * S], BF16, tag="p_grouped", align_bytes=64, name="p_grouped")
+                normalise(it, h, 2, half_done[it], at)
+                if at + 2 == QUAD:
+                    to_quantise.append((it, quad, half_done[it]))
+                room -= 1
+            if v_head is not None:
+                v_grouped = add_bias(v_head, accs[v_head])
             if k < STEPS:
-                h = (k - HS_STEPS) // 2
+                head = (k - HS_STEPS) // 2
                 if k >= HS_STEPS and (k - HS_STEPS) % 2 == 0:
-                    weights[h] = (
+                    weights[head] = (
                         work.tile([P, PASSES * HD], U32, tag="w_codes", align_bytes=64, name="w_codes"),
                         work.tile([P, PASSES * HD], U8, tag="w_scales", align_bytes=64, name="w_scales"),
                     )
-                w_codes, w_scales = weights.get(h, (None, None))
-                quantise_step(k, grouped[k], w_codes, w_scales)
-            if FIRST_PROJECT <= k < FIRST_PROJECT + 2 * H:
-                h, second = divmod(k - FIRST_PROJECT, 2)
-                if second == 0:
-                    accs[h] = psum.tile([P, BANK], F32, tag="acc", bufs=2, name="acc")
-                w_codes, w_scales = weights[h]
-                project_groups(accs[h], 2 * second, w_codes, w_scales)
-            if softmax_turn:
-                u += 1
-        for h in range(H):
-            attend(h)
+                quantise_step(k, grouped[k], *weights.get(head, (None, None)))
+            if v_head is not None:
+                quantise_v(v_head, v_grouped)
+                v_ready.add(v_head)
+            if k == STEPS:
+                part = bias_and_part(LAST, accs[LAST])
+                last_acc = psum.tile([P, BANK], F32, tag="acc", bufs=2, name="acc")
+                for t in range(ROW_TILES):
+                    project(last_acc, t, *weights[LAST], HALVES[1])
+                v_grouped = add_part(last_acc, part)
+                quantise_v(LAST, v_grouped)
+                v_ready.add(LAST)
+            for h in (attended, attended + 1):
+                if h == attended and h in v_ready and probs_ready.get(h // QUAD, 0) == ROW_TILES:
+                    attend(h)
+                    attended += 1

@@ -32,6 +32,7 @@ STEPS = HS_STEPS + WV_STEPS
 UNITS = ROW_TILES * ROW_TILES
 AHEAD = 2
 BATCH = 2
+WARM = 10
 QUAD = 4
 
 FLOPS = 2 * S * A * D + 2 * 2 * H * S * S * HD
@@ -90,6 +91,9 @@ def tile_sparseattention_pb_k_kernel(tc, q_rot, k_rot, hidden_states, Wv, bv, ou
                 nc.tensor.transpose(bank[:, h * P : (h + 1) * P], raw[:, h * HD : (h + 1) * HD], ident_bf16[:])
             copy(out=dst, in_=bank[:])
 
+        def keep_busy(bank):
+            nc.tensor.matmul(out=bank[:], lhsT=ident_bf16[:], rhs=kT[:, 0:BANK], start=True, stop=True)
+
         def transpose_step(s, raw):
             words = raw[:].bitcast(F32)
             halves = []
@@ -99,6 +103,8 @@ def tile_sparseattention_pb_k_kernel(tc, q_rot, k_rot, hidden_states, Wv, bv, ou
                     halves.append(grouped)
                 grouped_words = halves[-1][:].bitcast(F32)
                 bank = psum.tile([P, BANK], F32, tag="tp", bufs=4)
+                if s < WARM and b % 2 == 0:
+                    keep_busy(bank)
                 for a in range(2):
                     for u in range(2):
                         if s < HS_STEPS:
@@ -182,6 +188,8 @@ def tile_sparseattention_pb_k_kernel(tc, q_rot, k_rot, hidden_states, Wv, bv, ou
         def scores(unit):
             it, t = divmod(unit, ROW_TILES)
             score_banks[unit] = [psum.tile([P, BANK], F32, tag="sc", bufs=2, name="sc") for g in range(2)]
+            if unit < WARM:
+                keep_busy(score_banks[unit][1])
             for h in range(H):
                 for g in range(2):
                     first = h * P + g * HALF

@@ -201,6 +201,9 @@ def tile_sparseattention_pb_k_kernel(tc, q_rot, k_rot, hidden_states, Wv, bv, ou
                         stop=True,
                     )
 
+        def unit_cells(it, t):
+            return expd[it][:].rearrange("p (h c t i) -> p t h c i", h=H, t=ROW_TILES, i=4)[:, t]
+
         def subtract_max(unit):
             it, t = divmod(unit, ROW_TILES)
             banks = score_banks[unit]
@@ -214,51 +217,50 @@ def tile_sparseattention_pb_k_kernel(tc, q_rot, k_rot, hidden_states, Wv, bv, ou
                 )
             if t == 0:
                 expd[it] = work.tile([P, ROW_TILES * A], F32, tag="expd", bufs=4, name="expd")
-            unit_cols = expd[it][:, t * A : (t + 1) * A].rearrange("p (h i) -> p h i", h=H)
+            cells = unit_cells(it, t)
             for g in range(2):
                 nc.vector.tensor_tensor(
-                    out=unit_cols[:, :, g * HALF : (g + 1) * HALF],
-                    in0=banks[g][:].rearrange("p (h i) -> p h i", h=H),
-                    in1=top[:, g * HALF : (g + 1) * HALF].unsqueeze(1).to_broadcast([P, H, HALF]),
+                    out=cells[:, :, g * HALF // 4 : (g + 1) * HALF // 4],
+                    in0=banks[g][:].rearrange("p (h c i) -> p h c i", h=H, i=4),
+                    in1=top[:, g * HALF : (g + 1) * HALF]
+                    .rearrange("p (c i) -> p c i", i=4)
+                    .unsqueeze(1)
+                    .to_broadcast([P, H, HALF // 4, 4]),
                     op=ALU.subtract,
                 )
 
         def exp_and_sum(unit):
             it, t = divmod(unit, ROW_TILES)
             batch, member = divmod(it, BATCH)
-            unit_cols = expd[it][:, t * A : (t + 1) * A]
-            nc.scalar.activation(out=unit_cols, in_=unit_cols, func=ACT.Exp)
+            cells = unit_cells(it, t).rearrange("p h c i -> p (h c) i")
+            nc.scalar.activation(out=cells, in_=cells, func=ACT.Exp)
             if member == 0 and t == 0:
                 totals[batch] = work.tile([P, BATCH * ROW_TILES * P], F32, tag="totals", name="totals")
             part = work.tile([P, 4 * P], F32, tag="part", bufs=1)
-            first = (member * ROW_TILES + t) * P
-            nc.gpsimd.tensor_tensor(out=part[:], in0=unit_cols[:, 0 : 4 * P], in1=unit_cols[:, 4 * P : 8 * P], op=ALU.add)
+            sums = totals[batch][:, member * S : (member + 1) * S].rearrange("p (c t i) -> p t c i", t=ROW_TILES, i=4)[:, t]
+            part_cells = part[:].rearrange("p (c i) -> p c i", i=4)
+            half = P // 4 * H // 2
+            nc.gpsimd.tensor_tensor(out=part_cells, in0=cells[:, 0:half], in1=cells[:, half : 2 * half], op=ALU.add)
             nc.gpsimd.tensor_tensor(out=part[:, 0 : 2 * P], in0=part[:, 0 : 2 * P], in1=part[:, 2 * P : 4 * P], op=ALU.add)
-            nc.gpsimd.tensor_tensor(out=totals[batch][:, first : first + P], in0=part[:, 0:P], in1=part[:, P : 2 * P], op=ALU.add)
+            quarter = P // 4
+            nc.gpsimd.tensor_tensor(out=sums, in0=part_cells[:, 0:quarter], in1=part_cells[:, quarter : 2 * quarter], op=ALU.add)
 
         def log_sums(batch):
             nc.scalar.activation(out=totals[batch][:], in_=totals[batch][:], func=ACT.Ln)
 
         def invert_sums(batch):
             inverse[batch] = work.tile([P, BATCH * P * PACK], F32, tag="inverse", name="inverse")
-            for member in range(BATCH):
-                cols = slice(member * S, (member + 1) * S)
-                nc.scalar.activation(
-                    out=inverse[batch][:, cols].rearrange("p (i t) -> p i t", t=PACK),
-                    in_=totals[batch][:, cols].rearrange("p (t i) -> p i t", t=PACK),
-                    func=ACT.Exp,
-                    scale=-1.0,
-                )
+            nc.scalar.activation(out=inverse[batch][:], in_=totals[batch][:], func=ACT.Exp, scale=-1.0)
 
         def normalise(it, h, heads, p_grouped, at):
             batch, member = divmod(it, BATCH)
             nc.vector.tensor_tensor(
-                out=p_grouped[:, at * S : (at + heads) * S].rearrange("p (h i t) -> p h i t", h=heads, t=PACK),
-                in0=expd[it][:].rearrange("p (t h i) -> p h i t", t=PACK, h=H)[:, h : h + heads],
+                out=p_grouped[:, at * S : (at + heads) * S].rearrange("p (h c i t) -> p h c t i", h=heads, i=4, t=PACK),
+                in0=expd[it][:, h * S : (h + heads) * S].rearrange("p (h c t i) -> p h c t i", h=heads, i=4, t=PACK),
                 in1=inverse[batch][:, member * S : (member + 1) * S]
-                .rearrange("p (i t) -> p i t", t=PACK)
+                .rearrange("p (c t i) -> p c t i", t=PACK, i=4)
                 .unsqueeze(1)
-                .to_broadcast([P, heads, P, PACK]),
+                .to_broadcast([P, heads, P // 4, PACK, 4]),
                 op=ALU.mult,
             )
 

@@ -24,15 +24,15 @@ ROW_TILES = S // P
 PASSES = D // K_PASS
 BANK = 512
 HALF = BANK // H
+RUN = 4
+RUNS = P // RUN
 RAW = 4096
-GROUPED = RAW // 2
 HS_STEPS = S * D // (P * RAW)
-WV_STEPS = A * D // (P * RAW)
-STEPS = HS_STEPS + WV_STEPS
+STEPS = HS_STEPS + A * D // (P * RAW)
 UNITS = ROW_TILES * ROW_TILES
 AHEAD = 2
-BATCH = 2
-WARM = 10
+BATCHES = ((0, 1), (2, 3))
+BATCH_OF = {it: (b, its.index(it)) for b, its in enumerate(BATCHES) for it in its}
 QUAD = 4
 
 FLOPS = 2 * S * A * D + 2 * 2 * H * S * S * HD
@@ -51,6 +51,9 @@ def tile_sparseattention_pb_k_kernel(tc, q_rot, k_rot, hidden_states, Wv, bv, ou
         hs_rows = hidden_states.flatten_outer_dims().rearrange("(p t) k -> p t k", t=ROW_TILES)
         out_heads = out.flatten_outer_dims().rearrange("(h a) (b x) -> h (a b) x", h=H, b=2)
 
+        warm = keep.tile([P, 1], F32)
+        nc.vector.memset(warm[:], 0.0)
+        nc.scalar.activation(out=warm[:], in_=warm[:], func=ACT.Exp)
         ident_bf16 = keep.tile([P, P], BF16)
         make_identity(nc, ident_bf16[:])
         ident_f32 = keep.tile([P, P], F32)
@@ -65,18 +68,21 @@ def tile_sparseattention_pb_k_kernel(tc, q_rot, k_rot, hidden_states, Wv, bv, ou
         v_codes = keep.tile([P, A], U32, align_bytes=64)
         v_scales = keep.tile([P, A], U8, align_bytes=64)
 
-        def load_step(s, pieces=1):
+        stream = [("hs", i) for i in range(HS_STEPS)] + [("w", h, half) for h in range(H) for half in range(2)]
+
+        def load_step(k, pieces=1):
             raw = work.tile([P, RAW], BF16, tag="raw", bufs=AHEAD + 1)
-            if s < HS_STEPS:
+            step = stream[k]
+            if step[0] == "hs":
                 width = RAW // ROW_TILES
-                view = hs_rows[:, :, s * width : (s + 1) * width]
+                view = hs_rows[:, :, step[1] * width : (step[1] + 1) * width]
                 dst = raw[:].rearrange("p (t c) -> p t c", t=ROW_TILES)
                 piece = width // pieces
                 for i in range(pieces):
                     cols = slice(i * piece, (i + 1) * piece)
                     nc.sync.dma_start(out=dst[:, :, cols], in_=view[:, :, cols])
             else:
-                h, half = divmod(s - HS_STEPS, 2)
+                h, half = step[1:]
                 nc.sync.dma_start(out=raw[:], in_=Wv[h * HD : (h + 1) * HD, half * RAW : (half + 1) * RAW])
             return raw
 
@@ -91,86 +97,65 @@ def tile_sparseattention_pb_k_kernel(tc, q_rot, k_rot, hidden_states, Wv, bv, ou
                 nc.tensor.transpose(bank[:, h * P : (h + 1) * P], raw[:, h * HD : (h + 1) * HD], ident_bf16[:])
             copy(out=dst, in_=bank[:])
 
-        def keep_busy(bank):
-            nc.tensor.matmul(out=bank[:], lhsT=ident_bf16[:], rhs=kT[:, 0:BANK], start=True, stop=True)
-
-        def transpose_step(s, raw):
+        def transpose_step(k, raw, copies):
             words = raw[:].bitcast(F32)
-            halves = []
+            grouped = work.tile([P, RAW // 2], F32, tag="grouped", bufs=2, align_bytes=64)
             for b in range(RAW // 2 // BANK):
-                if b % 2 == 0:
-                    grouped = work.tile([P, GROUPED], BF16, tag="grouped", bufs=3, align_bytes=64)
-                    halves.append(grouped)
-                grouped_words = halves[-1][:].bitcast(F32)
                 bank = psum.tile([P, BANK], F32, tag="tp", bufs=4)
-                if s < WARM and b % 2 == 0:
-                    keep_busy(bank)
                 for a in range(2):
                     for u in range(2):
-                        if s < HS_STEPS:
+                        if stream[k][0] == "hs":
                             blk = (2 * (b % 2) + a) * 4 + (b // 2) * 2 + u
                         else:
                             blk = 4 * b + 2 * a + u
                         slot = (2 * a + u) * P
                         nc.tensor.transpose(bank[:, slot : slot + P], words[:, blk * P : (blk + 1) * P], ident_f32[:])
-                nc.scalar.copy(
-                    out=grouped_words[:, (b % 2) * BANK : (b % 2 + 1) * BANK].rearrange("p (a r u) -> p a r u", a=2, u=2),
+                copies[b](
+                    out=grouped[:, b * BANK : (b + 1) * BANK].rearrange("p (a r u) -> p a r u", a=2, u=2),
                     in_=bank[:].rearrange("p (a u r) -> p a r u", a=2, u=2),
                 )
-            return halves
+            return grouped
 
-        def quantise_step(s, halves, w_codes, w_scales):
-            for i, grouped in enumerate(halves):
-                width = GROUPED // PACK
-                if s < HS_STEPS:
-                    first = s * (RAW // PACK) + i * width
-                    codes, scales = hs_codes, hs_scales
-                else:
-                    first = ((s - HS_STEPS) % 2) * (RAW // PACK) + i * width
-                    codes, scales = w_codes, w_scales
-                cols = slice(first, first + width)
-                nc.vector.quantize_mx(out=codes[:, cols].bitcast(FP8X4), scales=scales[:, cols], in_=grouped[:])
+        weights = {}
 
-        def project(acc, t, w_codes, w_scales, passes):
-            for c in passes:
+        def quantise_step(k, grouped):
+            step = stream[k]
+            if step[0] == "hs":
+                codes, scales, first = hs_codes, hs_scales, step[1] * (RAW // PACK)
+            else:
+                codes = work.tile([P, RAW // PACK], U32, tag="w_codes", bufs=4, align_bytes=64, name="w_codes")
+                scales = work.tile([P, RAW // PACK], U8, tag="w_scales", bufs=4, align_bytes=64, name="w_scales")
+                weights[step[1:]] = (codes, scales)
+                first = 0
+            cols = slice(first, first + RAW // PACK)
+            nc.vector.quantize_mx(out=codes[:, cols].bitcast(FP8X4), scales=scales[:, cols], in_=grouped[:].bitcast(BF16))
+
+        accs = {}
+
+        def project(h, t):
+            if t == 0:
+                accs[h] = psum.tile([P, BANK], F32, tag="acc", bufs=2, name="acc")
+            for c in range(PASSES):
+                half, i = divmod(c, PASSES // 2)
+                w_codes, w_scales = weights[h, half]
                 hs_cols = slice(c * S + t * P, c * S + (t + 1) * P)
-                w_cols = slice(c * HD, (c + 1) * HD)
+                w_cols = slice(i * HD, (i + 1) * HD)
                 nc.tensor.matmul_mx(
-                    out=acc[:, t * HD : (t + 1) * HD],
+                    out=accs[h][:, t * HD : (t + 1) * HD],
                     lhsT=hs_codes[:, hs_cols].bitcast(FP8X4),
                     lhsT_scale=hs_scales[:, hs_cols],
                     rhs=w_codes[:, w_cols].bitcast(FP8X4),
                     rhs_scale=w_scales[:, w_cols],
-                    start=(c == passes[0]),
-                    stop=(c == passes[-1]),
+                    start=(c == 0),
+                    stop=(c == PASSES - 1),
                 )
 
-        def add_bias(h, acc):
-            v_grouped = work.tile([P, HD * PACK], BF16, tag="v_grouped", align_bytes=64)
+        def add_bias(h):
+            v_grouped = work.tile([P, HD * PACK], BF16, tag="v_grouped", align_bytes=64, name="v_grouped")
             nc.vector.tensor_tensor(
                 out=v_grouped[:].rearrange("p (d t) -> p d t", t=PACK),
-                in0=acc[:].rearrange("p (t d) -> p d t", t=PACK),
+                in0=accs[h][:].rearrange("p (t d) -> p d t", t=PACK),
                 in1=bias[:, h * HD : (h + 1) * HD].unsqueeze(2).to_broadcast([P, HD, PACK]),
-                op=ALU.add,
-            )
-            return v_grouped
-
-        def bias_and_part(h, acc):
-            part = work.tile([P, BANK], F32, tag="result", bufs=2)
-            nc.vector.tensor_tensor(
-                out=part[:].rearrange("p (t d) -> p t d", t=PACK),
-                in0=acc[:].rearrange("p (t d) -> p t d", t=PACK),
-                in1=bias[:, h * HD : (h + 1) * HD].unsqueeze(1).to_broadcast([P, PACK, HD]),
-                op=ALU.add,
-            )
-            return part
-
-        def add_part(acc, part):
-            v_grouped = work.tile([P, HD * PACK], BF16, tag="v_grouped", align_bytes=64)
-            nc.vector.tensor_tensor(
-                out=v_grouped[:].rearrange("p (d t) -> p d t", t=PACK),
-                in0=acc[:].rearrange("p (t d) -> p d t", t=PACK),
-                in1=part[:].rearrange("p (t d) -> p d t", t=PACK),
                 op=ALU.add,
             )
             return v_grouped
@@ -183,15 +168,12 @@ def tile_sparseattention_pb_k_kernel(tc, q_rot, k_rot, hidden_states, Wv, bv, ou
         qT = {}
         expd = {}
         totals = {}
-        inverse = {}
 
         def scores(unit):
             it, t = divmod(unit, ROW_TILES)
             score_banks[unit] = [psum.tile([P, BANK], F32, tag="sc", bufs=2, name="sc") for g in range(2)]
-            if unit < WARM:
-                keep_busy(score_banks[unit][1])
-            for h in range(H):
-                for g in range(2):
+            for g in range(2):
+                for h in range(H):
                     first = h * P + g * HALF
                     nc.tensor.matmul(
                         out=score_banks[unit][g][:, h * HALF : (h + 1) * HALF],
@@ -202,7 +184,7 @@ def tile_sparseattention_pb_k_kernel(tc, q_rot, k_rot, hidden_states, Wv, bv, ou
                     )
 
         def unit_cells(it, t):
-            return expd[it][:].rearrange("p (h c t i) -> p t h c i", h=H, t=ROW_TILES, i=4)[:, t]
+            return expd[it][:].rearrange("p (h c t i) -> p t h c i", h=H, t=ROW_TILES, i=RUN)[:, t]
 
         def subtract_max(unit):
             it, t = divmod(unit, ROW_TILES)
@@ -220,56 +202,55 @@ def tile_sparseattention_pb_k_kernel(tc, q_rot, k_rot, hidden_states, Wv, bv, ou
             cells = unit_cells(it, t)
             for g in range(2):
                 nc.vector.tensor_tensor(
-                    out=cells[:, :, g * HALF // 4 : (g + 1) * HALF // 4],
-                    in0=banks[g][:].rearrange("p (h c i) -> p h c i", h=H, i=4),
+                    out=cells[:, :, g * RUNS // 2 : (g + 1) * RUNS // 2],
+                    in0=banks[g][:].rearrange("p (h c i) -> p h c i", h=H, i=RUN),
                     in1=top[:, g * HALF : (g + 1) * HALF]
-                    .rearrange("p (c i) -> p c i", i=4)
+                    .rearrange("p (c i) -> p c i", i=RUN)
                     .unsqueeze(1)
-                    .to_broadcast([P, H, HALF // 4, 4]),
+                    .to_broadcast([P, H, RUNS // 2, RUN]),
                     op=ALU.subtract,
                 )
 
-        def exp_and_sum(unit):
+        def exp_and_sum(unit, scratch):
             it, t = divmod(unit, ROW_TILES)
-            batch, member = divmod(it, BATCH)
+            batch, member = BATCH_OF[it]
             cells = unit_cells(it, t).rearrange("p h c i -> p (h c) i")
             nc.scalar.activation(out=cells, in_=cells, func=ACT.Exp)
             if member == 0 and t == 0:
-                totals[batch] = work.tile([P, BATCH * ROW_TILES * P], F32, tag="totals", name="totals")
-            part = work.tile([P, 4 * P], F32, tag="part", bufs=1)
-            sums = totals[batch][:, member * S : (member + 1) * S].rearrange("p (c t i) -> p t c i", t=ROW_TILES, i=4)[:, t]
-            part_cells = part[:].rearrange("p (c i) -> p c i", i=4)
-            half = P // 4 * H // 2
-            nc.gpsimd.tensor_tensor(out=part_cells, in0=cells[:, 0:half], in1=cells[:, half : 2 * half], op=ALU.add)
+                totals[batch] = work.tile([P, len(BATCHES[batch]) * S], F32, tag="totals%d" % batch, bufs=1, name="totals")
+            part = scratch
+            sums = totals[batch][:, member * S : (member + 1) * S].rearrange("p (c t i) -> p t c i", t=ROW_TILES, i=RUN)[:, t]
+            fours = part[:, 0 : 4 * P].rearrange("p (c i) -> p c i", i=RUN)
+            half = RUNS * H // 2
+            nc.gpsimd.tensor_tensor(out=fours, in0=cells[:, 0:half], in1=cells[:, half : 2 * half], op=ALU.add)
             nc.gpsimd.tensor_tensor(out=part[:, 0 : 2 * P], in0=part[:, 0 : 2 * P], in1=part[:, 2 * P : 4 * P], op=ALU.add)
-            quarter = P // 4
-            nc.gpsimd.tensor_tensor(out=sums, in0=part_cells[:, 0:quarter], in1=part_cells[:, quarter : 2 * quarter], op=ALU.add)
+            last = dict(out=sums, in0=fours[:, 0:RUNS], in1=fours[:, RUNS : 2 * RUNS], op=ALU.add)
+            return last
 
         def log_sums(batch):
             nc.scalar.activation(out=totals[batch][:], in_=totals[batch][:], func=ACT.Ln)
 
         def invert_sums(batch):
-            inverse[batch] = work.tile([P, BATCH * P * PACK], F32, tag="inverse", name="inverse")
-            nc.scalar.activation(out=inverse[batch][:], in_=totals[batch][:], func=ACT.Exp, scale=-1.0)
+            nc.scalar.activation(out=totals[batch][:], in_=totals[batch][:], func=ACT.Exp, scale=-1.0)
 
         def normalise(it, h, heads, p_grouped, at):
-            batch, member = divmod(it, BATCH)
+            batch, member = BATCH_OF[it]
             nc.vector.tensor_tensor(
-                out=p_grouped[:, at * S : (at + heads) * S].rearrange("p (h c i t) -> p h c t i", h=heads, i=4, t=PACK),
-                in0=expd[it][:, h * S : (h + heads) * S].rearrange("p (h c t i) -> p h c t i", h=heads, i=4, t=PACK),
-                in1=inverse[batch][:, member * S : (member + 1) * S]
-                .rearrange("p (c t i) -> p c t i", t=PACK, i=4)
+                out=p_grouped[:, at * S : (at + heads) * S].rearrange("p (h c i t) -> p h c t i", h=heads, i=RUN, t=PACK),
+                in0=expd[it][:, h * S : (h + heads) * S].rearrange("p (h c t i) -> p h c t i", h=heads, i=RUN, t=PACK),
+                in1=totals[batch][:, member * S : (member + 1) * S]
+                .rearrange("p (c t i) -> p c t i", t=PACK, i=RUN)
                 .unsqueeze(1)
-                .to_broadcast([P, heads, P // 4, PACK, 4]),
+                .to_broadcast([P, heads, RUNS, PACK, RUN]),
                 op=ALU.mult,
             )
 
-        def quantise_probs(it, quad, p_grouped):
-            first = it * A + quad * QUAD * P
-            cols = slice(first, first + QUAD * P)
+        def quantise_probs(it, heads, p_grouped):
+            first = it * A + heads[0] * P
+            cols = slice(first, first + len(heads) * P)
             nc.vector.quantize_mx(out=p_codes[:, cols].bitcast(FP8X4), scales=p_scales[:, cols], in_=p_grouped[:])
 
-        def attend(h):
+        def attend(h, copy):
             acc = psum.tile([P, BANK], F32, tag="sc", bufs=2, name="attended")
             for it in range(ROW_TILES):
                 p_cols = slice(it * A + h * P, it * A + (h + 1) * P)
@@ -283,8 +264,8 @@ def tile_sparseattention_pb_k_kernel(tc, q_rot, k_rot, hidden_states, Wv, bv, ou
                     start=True,
                     stop=True,
                 )
-            result = work.tile([P, BANK], F32, tag="result", bufs=2)
-            nc.scalar.copy(out=result[:], in_=acc[:])
+            result = work.tile([P, BANK], F32, tag="result", bufs=3)
+            copy(out=result[:], in_=acc[:])
             nc.sync.dma_start(out=out_heads[h], in_=result[:])
 
         raws = {}
@@ -292,116 +273,114 @@ def tile_sparseattention_pb_k_kernel(tc, q_rot, k_rot, hidden_states, Wv, bv, ou
         q_raw = {}
         k_raw[0] = load_rows(k_rows, 0)
         q_raw[0] = load_rows(q_rows, 0)
-        raws[0] = load_step(0, pieces=2)
         k_raw[1] = load_rows(k_rows, 1)
+        raws[0] = load_step(0, pieces=2)
         raws[1] = load_step(1)
         transpose_rows(k_raw[0], kT[:, 0:A], nc.scalar.copy)
         qT[0] = work.tile([P, A], BF16, tag="qT", name="qT")
         transpose_rows(q_raw[0], qT[0][:], nc.vector.tensor_copy)
-        scores(0)
-        for t in range(2, ROW_TILES):
-            k_raw[t] = load_rows(k_rows, t)
+        transpose_rows(k_raw[1], kT[:, A : 2 * A], nc.vector.tensor_copy)
+        k_raw[2] = load_rows(k_rows, 2)
+        k_raw[3] = load_rows(k_rows, 3)
 
-        FIRST_PROJECT = HS_STEPS + 2
-        LAST = H - 1
-        HALVES = (range(PASSES // 2), range(PASSES // 2, PASSES))
-        units_of_batch = BATCH * ROW_TILES
-
-        loaded = {}
+        UNIT_AT = list(range(UNITS))
+        GROUPS = ((0, 1, 2, 3), (4, 5, 6, 7))
+        last_unit = UNIT_AT[-1]
+        batch_end = [UNIT_AT[(its[-1] + 1) * ROW_TILES - 1] for its in BATCHES]
         grouped = {}
-        weights = {}
-        accs = {}
-        normal_queue = []
-        half_done = {}
+        jobs = []
+        biasing = []
+        quantising = []
+        chunks = []
+        filled = {}
         to_quantise = []
         probs_ready = {}
         v_ready = set()
         attended = 0
-        for k in range(STEPS + 3):
-            if k % ROW_TILES == 1 and k // ROW_TILES + 1 < ROW_TILES:
-                q_raw[k // ROW_TILES + 1] = load_rows(q_rows, k // ROW_TILES + 1)
+        to_exp = []
+        adds = []
+        for k in range(STEPS + 5):
             if k + AHEAD < STEPS:
                 raws[k + AHEAD] = load_step(k + AHEAD)
+            units = [u for u in range(UNITS) if UNIT_AT[u] == k]
+            for it in range(1, ROW_TILES):
+                if k == max(1, UNIT_AT[it * ROW_TILES] - 4):
+                    q_raw[it] = load_rows(q_rows, it)
             if k == ROW_TILES:
                 nc.sync.dma_start(out=bias[:], in_=bv.partition_broadcast(P))
-
-            if k < UNITS:
-                subtract_max(k)
+            if 0 < k <= STEPS:
+                quantise_step(k - 1, grouped[k - 1])
+                if stream[k - 1][0] == "w" and stream[k - 1][2] == 1:
+                    h = stream[k - 1][1]
+                    jobs += [(k, h, 0), (k, h, 1), (k + 1 - (k == STEPS), h, 2), (k + 1 - (k == STEPS), h, 3)]
+            for h, v_grouped in quantising:
+                quantise_v(h, v_grouped)
+                v_ready.add(h)
+            quantising = []
+            if units:
+                scores(units[0])
+            adds_now = adds
+            adds = []
+            for u in to_exp:
+                adds.append(exp_and_sum(u, grouped[min(k, STEPS) - 1]))
+            to_exp = units
             if k < STEPS:
-                grouped[k] = transpose_step(k, raws[k])
-            if k + 1 < ROW_TILES:
-                transpose_rows(k_raw[k + 1], kT[:, (k + 1) * A : (k + 2) * A], nc.scalar.copy)
-            if (k + 1) % ROW_TILES == 0 and k + 1 < UNITS:
-                it = (k + 1) // ROW_TILES
-                qT[it] = work.tile([P, A], BF16, tag="qT", name="qT")
-                transpose_rows(q_raw[it], qT[it][:], nc.scalar.copy)
-
-            head, second = divmod(k - FIRST_PROJECT, 2)
-            projecting = 0 <= head < LAST
-            if projecting:
-                if second == 0:
-                    accs[head] = psum.tile([P, BANK], F32, tag="acc", bufs=2, name="acc")
-                project(accs[head], 2 * second, *weights[head], range(PASSES))
-            if k + 1 < UNITS:
-                scores(k + 1)
-            if projecting:
-                project(accs[head], 2 * second + 1, *weights[head], range(PASSES))
-            if k == STEPS - 1:
-                accs[LAST] = psum.tile([P, BANK], F32, tag="acc", bufs=2, name="acc")
-                for t in range(ROW_TILES):
-                    project(accs[LAST], t, *weights[LAST], HALVES[0])
-
-            if k < UNITS:
-                exp_and_sum(k)
-            for batch in range(ROW_TILES // BATCH):
-                if k == (batch + 1) * units_of_batch:
-                    log_sums(batch)
-                if k == (batch + 1) * units_of_batch + 1:
-                    invert_sums(batch)
-                    for quad in range(H // QUAD):
-                        for it in range(batch * BATCH, (batch + 1) * BATCH):
-                            for h in range(quad * QUAD, (quad + 1) * QUAD, 2):
-                                normal_queue.append((it, h, k + 1))
-
-            for it, quad, p_grouped in to_quantise:
-                quantise_probs(it, quad, p_grouped)
-                probs_ready[quad] = probs_ready.get(quad, 0) + 1
+                grouped[k] = transpose_step(k, raws[k], [nc.scalar.copy] * 4)
+            for b, its in enumerate(BATCHES):
+                if k == batch_end[b] + 3:
+                    log_sums(b)
+                if k == batch_end[b] + 4:
+                    invert_sums(b)
+                    for heads in GROUPS:
+                        for it in its:
+                            for i in range(0, len(heads), 2):
+                                chunks.append((it, heads, i, k + 1))
+            for u in range(2, UNITS):
+                it, t = divmod(u, ROW_TILES)
+                if UNIT_AT[u] - 2 == k:
+                    if it == 0:
+                        transpose_rows(k_raw[t], kT[:, t * A : (t + 1) * A], nc.scalar.copy)
+                    elif t == 0:
+                        qT[it] = work.tile([P, A], BF16, tag="qT", name="qT")
+                        transpose_rows(q_raw[it], qT[it][:], nc.scalar.copy)
+            for i, u in enumerate(units):
+                if i > 0:
+                    scores(u)
+                subtract_max(u)
+            for last in adds_now:
+                if last is not None:
+                    nc.vector.tensor_tensor(**last)
+            for h in biasing:
+                quantising.append((h, add_bias(h)))
+            biasing = []
+            for it, heads, p_grouped in to_quantise:
+                quantise_probs(it, heads, p_grouped)
+                probs_ready[heads] = probs_ready.get(heads, 0) + 1
             to_quantise = []
-            v_head = (k - FIRST_PROJECT - 2) // 2 if k >= FIRST_PROJECT + 2 and (k - FIRST_PROJECT) % 2 == 0 else None
-            if v_head is not None and v_head >= LAST:
-                v_head = None
-            room = 2 if k >= UNITS else (1 if v_head is None else 0)
-            while room > 0 and normal_queue and normal_queue[0][2] <= k:
-                it, h, ready = normal_queue.pop(0)
-                quad, at = divmod(h, QUAD)
-                if at == 0:
-                    half_done[it] = work.tile([P, QUAD * S], BF16, tag="p_grouped", align_bytes=64, name="p_grouped")
-                normalise(it, h, 2, half_done[it], at)
-                if at + 2 == QUAD:
-                    to_quantise.append((it, quad, half_done[it]))
+            room = 2 if k > last_unit else 0
+            while room > 0 and chunks and chunks[0][3] <= k:
+                it, heads, i, ready = chunks.pop(0)
+                count = min(2, len(heads))
+                if i == 0:
+                    filled[it] = work.tile([P, len(heads) * S], BF16, tag="p_grouped", bufs=2, align_bytes=64, name="p_grouped")
+                normalise(it, heads[i], count, filled[it], i)
+                if i + count == len(heads):
+                    to_quantise.append((it, heads, filled[it]))
                 room -= 1
-            if v_head is not None:
-                v_grouped = add_bias(v_head, accs[v_head])
-            if k < STEPS:
-                head = (k - HS_STEPS) // 2
-                if k >= HS_STEPS and (k - HS_STEPS) % 2 == 0:
-                    weights[head] = (
-                        work.tile([P, PASSES * HD], U32, tag="w_codes", align_bytes=64, name="w_codes"),
-                        work.tile([P, PASSES * HD], U8, tag="w_scales", align_bytes=64, name="w_scales"),
-                    )
-                quantise_step(k, grouped[k], *weights.get(head, (None, None)))
-            if v_head is not None:
-                quantise_v(v_head, v_grouped)
-                v_ready.add(v_head)
-            if k == STEPS:
-                part = bias_and_part(LAST, accs[LAST])
-                last_acc = psum.tile([P, BANK], F32, tag="acc", bufs=2, name="acc")
-                for t in range(ROW_TILES):
-                    project(last_acc, t, *weights[LAST], HALVES[1])
-                v_grouped = add_part(last_acc, part)
-                quantise_v(LAST, v_grouped)
-                v_ready.add(LAST)
-            for h in (attended, attended + 1):
-                if h == attended and h in v_ready and probs_ready.get(h // QUAD, 0) == ROW_TILES:
-                    attend(h)
+            now = [j for j in jobs if j[0] <= k]
+            jobs = [j for j in jobs if j[0] > k]
+            for due, h, t in now:
+                project(h, t)
+                if t == ROW_TILES - 1:
+                    biasing.append(h)
+            if k > STEPS:
+                for h, v_grouped in quantising:
+                    quantise_v(h, v_grouped)
+                    v_ready.add(h)
+                quantising = []
+            for h in range(attended, H):
+                heads = [g for g in GROUPS if h in g][0]
+                if h == attended and h in v_ready and probs_ready.get(heads, 0) == ROW_TILES and h < attended + 2:
+                    attend(h, nc.scalar.copy)
                     attended += 1
+        assert attended == H

@@ -211,20 +211,22 @@ def tile_sparseattention_pb_k_kernel(tc, q_rot, k_rot, hidden_states, Wv, bv, ou
                     op=ALU.subtract,
                 )
 
-        def exp_and_sum(unit, scratch):
+        def exp_and_sum(unit):
             it, t = divmod(unit, ROW_TILES)
             batch, member = BATCH_OF[it]
             cells = unit_cells(it, t).rearrange("p h c i -> p (h c) i")
             nc.scalar.activation(out=cells, in_=cells, func=ACT.Exp)
             if member == 0 and t == 0:
                 totals[batch] = work.tile([P, len(BATCHES[batch]) * S], F32, tag="totals%d" % batch, bufs=1, name="totals")
-            part = scratch
+            part = work.tile([P, 4 * P], F32, tag="part", bufs=1)
             sums = totals[batch][:, member * S : (member + 1) * S].rearrange("p (c t i) -> p t c i", t=ROW_TILES, i=RUN)[:, t]
             fours = part[:, 0 : 4 * P].rearrange("p (c i) -> p c i", i=RUN)
             half = RUNS * H // 2
             nc.gpsimd.tensor_tensor(out=fours, in0=cells[:, 0:half], in1=cells[:, half : 2 * half], op=ALU.add)
-            nc.gpsimd.tensor_tensor(out=part[:, 0 : 2 * P], in0=part[:, 0 : 2 * P], in1=part[:, 2 * P : 4 * P], op=ALU.add)
-            last = dict(out=sums, in0=fours[:, 0:RUNS], in1=fours[:, RUNS : 2 * RUNS], op=ALU.add)
+            pair = work.tile([P, 2 * P], F32, tag="pair", bufs=2)
+            nc.gpsimd.tensor_tensor(out=pair[:], in0=part[:, 0 : 2 * P], in1=part[:, 2 * P : 4 * P], op=ALU.add)
+            twos = pair[:].rearrange("p (c i) -> p c i", i=RUN)
+            last = dict(out=sums, in0=twos[:, 0:RUNS], in1=twos[:, RUNS : 2 * RUNS], op=ALU.add)
             return last
 
         def log_sums(batch):
@@ -284,7 +286,7 @@ def tile_sparseattention_pb_k_kernel(tc, q_rot, k_rot, hidden_states, Wv, bv, ou
         k_raw[3] = load_rows(k_rows, 3)
 
         UNIT_AT = list(range(UNITS))
-        GROUPS = ((0, 1, 2, 3), (4, 5, 6, 7))
+        GROUPS = ((0, 1, 2, 3), (4, 5), (6, 7))
         last_unit = UNIT_AT[-1]
         batch_end = [UNIT_AT[(its[-1] + 1) * ROW_TILES - 1] for its in BATCHES]
         grouped = {}
@@ -322,7 +324,7 @@ def tile_sparseattention_pb_k_kernel(tc, q_rot, k_rot, hidden_states, Wv, bv, ou
             adds_now = adds
             adds = []
             for u in to_exp:
-                adds.append(exp_and_sum(u, grouped[min(k, STEPS) - 1]))
+                adds.append(exp_and_sum(u))
             to_exp = units
             if k < STEPS:
                 grouped[k] = transpose_step(k, raws[k], [nc.scalar.copy] * 4)

@@ -91,10 +91,12 @@ def tile_sparseattention_pb_k_kernel(tc, q_rot, k_rot, hidden_states, Wv, bv, ou
             nc.sync.dma_start(out=raw[:], in_=rows[:, t, :])
             return raw
 
-        def transpose_rows(raw, dst, copy):
+        def transpose_rows(raw, dst, copy=None):
             bank = psum.tile([P, A], BF16, tag="tp", bufs=4)
             for h in range(H):
                 nc.tensor.transpose(bank[:, h * P : (h + 1) * P], raw[:, h * HD : (h + 1) * HD], ident_bf16[:])
+            if copy is None:
+                return dst, bank
             copy(out=dst, in_=bank[:])
 
         def transpose_step(k, raw, copies):
@@ -308,7 +310,7 @@ def tile_sparseattention_pb_k_kernel(tc, q_rot, k_rot, hidden_states, Wv, bv, ou
             for it in range(1, ROW_TILES):
                 if k == max(1, UNIT_AT[it * ROW_TILES] - 4):
                     q_raw[it] = load_rows(q_rows, it)
-            if k == ROW_TILES:
+            if k == HS_STEPS + 1:
                 nc.sync.dma_start(out=bias[:], in_=bv.partition_broadcast(P))
             if 0 < k <= STEPS:
                 quantise_step(k - 1, grouped[k - 1])
@@ -331,24 +333,31 @@ def tile_sparseattention_pb_k_kernel(tc, q_rot, k_rot, hidden_states, Wv, bv, ou
             for b, its in enumerate(BATCHES):
                 if k == batch_end[b] + 3:
                     log_sums(b)
-                if k == batch_end[b] + 4:
+                if k == batch_end[b] + 5:
                     invert_sums(b)
                     for heads in GROUPS:
                         for it in its:
                             for i in range(0, len(heads), 2):
                                 chunks.append((it, heads, i, k + 1))
+            turned = []
             for u in range(2, UNITS):
                 it, t = divmod(u, ROW_TILES)
-                if UNIT_AT[u] - 2 == k:
+                if UNIT_AT[u] - 2 == k and (it == 0 or t == 0):
                     if it == 0:
-                        transpose_rows(k_raw[t], kT[:, t * A : (t + 1) * A], nc.scalar.copy)
-                    elif t == 0:
+                        raw, dst = k_raw[t], kT[:, t * A : (t + 1) * A]
+                    else:
                         qT[it] = work.tile([P, A], BF16, tag="qT", name="qT")
-                        transpose_rows(q_raw[it], qT[it][:], nc.scalar.copy)
+                        raw, dst = q_raw[it], qT[it][:]
+                    if it == 0 and t == 3:
+                        turned.append(transpose_rows(raw, dst))
+                    else:
+                        transpose_rows(raw, dst, nc.scalar.copy)
             for i, u in enumerate(units):
                 if i > 0:
                     scores(u)
                 subtract_max(u)
+            for dst, bank in turned:
+                nc.vector.tensor_copy(out=dst, in_=bank[:])
             for last in adds_now:
                 if last is not None:
                     nc.vector.tensor_tensor(**last)

@@ -268,7 +268,7 @@ def tile_sparseattention_pb_k_kernel(tc, q_rot, k_rot, hidden_states, Wv, bv, ou
                     start=True,
                     stop=True,
                 )
-            result = work.tile([P, BANK], F32, tag="result", bufs=3)
+            result = work.tile([P, BANK], F32, tag="result", bufs=5)
             copy(out=result[:], in_=acc[:])
             nc.sync.dma_start(out=out_heads[h], in_=result[:])
 
@@ -278,7 +278,7 @@ def tile_sparseattention_pb_k_kernel(tc, q_rot, k_rot, hidden_states, Wv, bv, ou
         k_raw[0] = load_rows(k_rows, 0)
         q_raw[0] = load_rows(q_rows, 0)
         k_raw[1] = load_rows(k_rows, 1)
-        raws[0] = load_step(0, pieces=2)
+        raws[0] = load_step(0, pieces=1)
         raws[1] = load_step(1)
         transpose_rows(k_raw[0], kT[:, 0:A], nc.scalar.copy)
         qT[0] = work.tile([P, A], BF16, tag="qT", name="qT")
@@ -288,7 +288,7 @@ def tile_sparseattention_pb_k_kernel(tc, q_rot, k_rot, hidden_states, Wv, bv, ou
         k_raw[3] = load_rows(k_rows, 3)
 
         UNIT_AT = list(range(UNITS))
-        GROUPS = ((0, 1, 2, 3), (4, 5), (6, 7))
+        GROUPS = ((0, 1), (2, 3), (4, 5), (6, 7))
         last_unit = UNIT_AT[-1]
         batch_end = [UNIT_AT[(its[-1] + 1) * ROW_TILES - 1] for its in BATCHES]
         grouped = {}
@@ -348,7 +348,7 @@ def tile_sparseattention_pb_k_kernel(tc, q_rot, k_rot, hidden_states, Wv, bv, ou
                     else:
                         qT[it] = work.tile([P, A], BF16, tag="qT", name="qT")
                         raw, dst = q_raw[it], qT[it][:]
-                    if it == 0 and t == 3:
+                    if it == 0 and t == 3 or it == 3:
                         turned.append(transpose_rows(raw, dst))
                     else:
                         transpose_rows(raw, dst, nc.scalar.copy)

@@ -59,6 +59,9 @@ def tile_sparseattention_pb_k_kernel(tc, q_rot, k_rot, hidden_states, Wv, bv, ou
         ident_f32 = keep.tile([P, P], F32)
         make_identity(nc, ident_f32[:])
         bias = keep.tile([P, A], BF16)
+        unread = psum.tile([P, BANK], F32, tag="sc", bufs=2, name="unread")
+        for i in range(16):
+            nc.tensor.matmul(out=unread[:, 0:P], lhsT=ident_bf16[:], rhs=ident_bf16[:], start=True, stop=True)
 
         kT = keep.tile([P, ROW_TILES * A], BF16)
         hs_codes = keep.tile([P, PASSES * S], U32, align_bytes=64)
@@ -99,7 +102,7 @@ def tile_sparseattention_pb_k_kernel(tc, q_rot, k_rot, hidden_states, Wv, bv, ou
                 return dst, bank
             copy(out=dst, in_=bank[:])
 
-        def transpose_step(k, raw, copies):
+        def transpose_step(k, raw, late):
             words = raw[:].bitcast(F32)
             grouped = work.tile([P, RAW // 2], F32, tag="grouped", bufs=2, align_bytes=64)
             for b in range(RAW // 2 // BANK):
@@ -112,12 +115,17 @@ def tile_sparseattention_pb_k_kernel(tc, q_rot, k_rot, hidden_states, Wv, bv, ou
                             blk = 4 * b + 2 * a + u
                         slot = (2 * a + u) * P
                         nc.tensor.transpose(bank[:, slot : slot + P], words[:, blk * P : (blk + 1) * P], ident_f32[:])
-                copies[b](
+                move = dict(
                     out=grouped[:, b * BANK : (b + 1) * BANK].rearrange("p (a r u) -> p a r u", a=2, u=2),
                     in_=bank[:].rearrange("p (a u r) -> p a r u", a=2, u=2),
                 )
+                if b < late:
+                    nc.scalar.copy(**move)
+                else:
+                    moves.append(move)
             return grouped
 
+        moves = []
         weights = {}
 
         def quantise_step(k, grouped):
@@ -170,6 +178,7 @@ def tile_sparseattention_pb_k_kernel(tc, q_rot, k_rot, hidden_states, Wv, bv, ou
         qT = {}
         expd = {}
         totals = {}
+        twos = {}
 
         def scores(unit):
             it, t = divmod(unit, ROW_TILES)
@@ -221,15 +230,18 @@ def tile_sparseattention_pb_k_kernel(tc, q_rot, k_rot, hidden_states, Wv, bv, ou
             if member == 0 and t == 0:
                 totals[batch] = work.tile([P, len(BATCHES[batch]) * S], F32, tag="totals%d" % batch, bufs=1, name="totals")
             part = work.tile([P, 4 * P], F32, tag="part", bufs=1)
-            sums = totals[batch][:, member * S : (member + 1) * S].rearrange("p (c t i) -> p t c i", t=ROW_TILES, i=RUN)[:, t]
+            sums = totals[batch][:, member * S : (member + 1) * S].rearrange("p (c t i) -> p t c i", t=ROW_TILES, i=RUN)[:, t - 1 : t + 1]
             fours = part[:, 0 : 4 * P].rearrange("p (c i) -> p c i", i=RUN)
             half = RUNS * H // 2
             nc.gpsimd.tensor_tensor(out=fours, in0=cells[:, 0:half], in1=cells[:, half : 2 * half], op=ALU.add)
-            pair = work.tile([P, 2 * P], F32, tag="pair", bufs=2)
-            nc.gpsimd.tensor_tensor(out=pair[:], in0=part[:, 0 : 2 * P], in1=part[:, 2 * P : 4 * P], op=ALU.add)
-            twos = pair[:].rearrange("p (c i) -> p c i", i=RUN)
-            last = dict(out=sums, in0=twos[:, 0:RUNS], in1=twos[:, RUNS : 2 * RUNS], op=ALU.add)
-            return last
+            if t % 2 == 0:
+                twos[it] = work.tile([P, 4 * P], F32, tag="twos", bufs=2, name="twos")
+            at = (t % 2) * 2 * P
+            nc.gpsimd.tensor_tensor(out=twos[it][:, at : at + 2 * P], in0=part[:, 0 : 2 * P], in1=part[:, 2 * P : 4 * P], op=ALU.add)
+            if t % 2 == 0:
+                return None
+            halves = twos[it][:].rearrange("p (u f c i) -> p u f c i", u=2, f=2, i=RUN)
+            return dict(out=sums, in0=halves[:, :, 0], in1=halves[:, :, 1], op=ALU.add)
 
         def log_sums(batch):
             nc.scalar.activation(out=totals[batch][:], in_=totals[batch][:], func=ACT.Ln)
@@ -268,7 +280,7 @@ def tile_sparseattention_pb_k_kernel(tc, q_rot, k_rot, hidden_states, Wv, bv, ou
                     start=True,
                     stop=True,
                 )
-            result = work.tile([P, BANK], F32, tag="result", bufs=5)
+            result = work.tile([P, BANK], F32, tag="result", bufs=4)
             copy(out=result[:], in_=acc[:])
             nc.sync.dma_start(out=out_heads[h], in_=result[:])
 
@@ -278,7 +290,7 @@ def tile_sparseattention_pb_k_kernel(tc, q_rot, k_rot, hidden_states, Wv, bv, ou
         k_raw[0] = load_rows(k_rows, 0)
         q_raw[0] = load_rows(q_rows, 0)
         k_raw[1] = load_rows(k_rows, 1)
-        raws[0] = load_step(0, pieces=1)
+        raws[0] = load_step(0)
         raws[1] = load_step(1)
         transpose_rows(k_raw[0], kT[:, 0:A], nc.scalar.copy)
         qT[0] = work.tile([P, A], BF16, tag="qT", name="qT")
@@ -329,7 +341,7 @@ def tile_sparseattention_pb_k_kernel(tc, q_rot, k_rot, hidden_states, Wv, bv, ou
                 adds.append(exp_and_sum(u))
             to_exp = units
             if k < STEPS:
-                grouped[k] = transpose_step(k, raws[k], [nc.scalar.copy] * 4)
+                grouped[k] = transpose_step(k, raws[k], 2 if k == batch_end[0] + 3 else 4)
             for b, its in enumerate(BATCHES):
                 if k == batch_end[b] + 3:
                     log_sums(b)
@@ -361,13 +373,16 @@ def tile_sparseattention_pb_k_kernel(tc, q_rot, k_rot, hidden_states, Wv, bv, ou
             for last in adds_now:
                 if last is not None:
                     nc.vector.tensor_tensor(**last)
-            for h in biasing:
-                quantising.append((h, add_bias(h)))
-            biasing = []
+            for move in moves:
+                nc.vector.tensor_copy(**move)
+            moves.clear()
             for it, heads, p_grouped in to_quantise:
                 quantise_probs(it, heads, p_grouped)
                 probs_ready[heads] = probs_ready.get(heads, 0) + 1
             to_quantise = []
+            for h in biasing:
+                quantising.append((h, add_bias(h)))
+            biasing = []
             room = 2 if k > last_unit else 0
             while room > 0 and chunks and chunks[0][3] <= k:
                 it, heads, i, ready = chunks.pop(0)

@@ -291,12 +291,12 @@ def tile_sparseattention_pb_k_kernel(tc, q_rot, k_rot, hidden_states, Wv, bv, ou
         q_raw[0] = load_rows(q_rows, 0)
         k_raw[1] = load_rows(k_rows, 1)
         raws[0] = load_step(0)
-        raws[1] = load_step(1)
         transpose_rows(k_raw[0], kT[:, 0:A], nc.scalar.copy)
         qT[0] = work.tile([P, A], BF16, tag="qT", name="qT")
         transpose_rows(q_raw[0], qT[0][:], nc.vector.tensor_copy)
-        transpose_rows(k_raw[1], kT[:, A : 2 * A], nc.vector.tensor_copy)
         k_raw[2] = load_rows(k_rows, 2)
+        raws[1] = load_step(1)
+        transpose_rows(k_raw[1], kT[:, A : 2 * A], nc.vector.tensor_copy)
         k_raw[3] = load_rows(k_rows, 3)
 
         UNIT_AT = list(range(UNITS))

@@ -102,10 +102,9 @@ def tile_sparseattention_pb_k_kernel(tc, q_rot, k_rot, hidden_states, Wv, bv, ou
                 return dst, bank
             copy(out=dst, in_=bank[:])
 
-        def transpose_step(k, raw, late):
+        def transpose_step(k, raw, late, grouped, banks):
             words = raw[:].bitcast(F32)
-            grouped = work.tile([P, RAW // 2], F32, tag="grouped", bufs=2, align_bytes=64)
-            for b in range(RAW // 2 // BANK):
+            for b in banks:
                 bank = psum.tile([P, BANK], F32, tag="tp", bufs=4)
                 for a in range(2):
                     for u in range(2):
@@ -123,7 +122,6 @@ def tile_sparseattention_pb_k_kernel(tc, q_rot, k_rot, hidden_states, Wv, bv, ou
                     nc.scalar.copy(**move)
                 else:
                     moves.append(move)
-            return grouped
 
         moves = []
         weights = {}
@@ -293,10 +291,10 @@ def tile_sparseattention_pb_k_kernel(tc, q_rot, k_rot, hidden_states, Wv, bv, ou
         raws[0] = load_step(0)
         transpose_rows(k_raw[0], kT[:, 0:A], nc.scalar.copy)
         qT[0] = work.tile([P, A], BF16, tag="qT", name="qT")
-        transpose_rows(q_raw[0], qT[0][:], nc.vector.tensor_copy)
+        transpose_rows(q_raw[0], qT[0][:], nc.scalar.copy)
         k_raw[2] = load_rows(k_rows, 2)
         raws[1] = load_step(1)
-        transpose_rows(k_raw[1], kT[:, A : 2 * A], nc.vector.tensor_copy)
+        transpose_rows(k_raw[1], kT[:, A : 2 * A], nc.scalar.copy)
         k_raw[3] = load_rows(k_rows, 3)
 
         UNIT_AT = list(range(UNITS))
@@ -333,15 +331,18 @@ def tile_sparseattention_pb_k_kernel(tc, q_rot, k_rot, hidden_states, Wv, bv, ou
                 quantise_v(h, v_grouped)
                 v_ready.add(h)
             quantising = []
-            if units:
-                scores(units[0])
             adds_now = adds
             adds = []
             for u in to_exp:
                 adds.append(exp_and_sum(u))
             to_exp = units
             if k < STEPS:
-                grouped[k] = transpose_step(k, raws[k], 2 if k == batch_end[0] + 3 else 4)
+                grouped[k] = work.tile([P, RAW // 2], F32, tag="grouped", bufs=2, align_bytes=64, name="grouped")
+                transpose_step(k, raws[k], 2 if k == batch_end[0] + 3 else 4, grouped[k], range(1))
+            if units:
+                scores(units[0])
+            if k < STEPS:
+                transpose_step(k, raws[k], 2 if k == batch_end[0] + 3 else 4, grouped[k], range(1, 4))
             for b, its in enumerate(BATCHES):
                 if k == batch_end[b] + 3:
                     log_sums(b)
@@ -383,7 +384,7 @@ def tile_sparseattention_pb_k_kernel(tc, q_rot, k_rot, hidden_states, Wv, bv, ou
             for h in biasing:
                 quantising.append((h, add_bias(h)))
             biasing = []
-            room = 2 if k > last_unit else 0
+            room = 2 if k > last_unit + 1 else (1 if k > last_unit else 0)
             while room > 0 and chunks and chunks[0][3] <= k:
                 it, heads, i, ready = chunks.pop(0)
                 count = min(2, len(heads))

from contextlib import ExitStack

import concourse.mybir as mybir
from concourse.masks import make_identity

F32 = mybir.dt.float32
BF16 = mybir.dt.bfloat16
U32 = mybir.dt.uint32
U8 = mybir.dt.uint8
FP8X4 = mybir.dt.float8_e4m3fn_x4
ALU = mybir.AluOpType
ACT = mybir.ActivationFunctionType
AXIS = mybir.AxisListType

P = 128
PACK = 4
K_PASS = P * PACK
S = 512
D = 8192
A = 1024
H = 8
HD = A // H
ROW_TILES = S // P
PASSES = D // K_PASS
BANK = 512
HALF = BANK // H
RUN = 4
RUNS = P // RUN
RAW = 4096
HS_STEPS = S * D // (P * RAW)
STEPS = HS_STEPS + A * D // (P * RAW)
UNITS = ROW_TILES * ROW_TILES
AHEAD = 2
BATCHES = ((0, 1), (2, 3))
BATCH_OF = {it: (b, its.index(it)) for b, its in enumerate(BATCHES) for it in its}
QUAD = 4

FLOPS = 2 * S * A * D + 2 * 2 * H * S * S * HD


def tile_sparseattention_pb_k_kernel(tc, q_rot, k_rot, hidden_states, Wv, bv, out):
    nc = tc.nc
    with ExitStack() as ctx:
        ctx.enter_context(tc.manual_schedule())
        keep = ctx.enter_context(tc.tile_pool(name="keep", bufs=1))
        work = ctx.enter_context(tc.tile_pool(name="work", bufs=2))
        psum = ctx.enter_context(tc.psum_pool(name="psum", bufs=2))

        q_rows = q_rot.flatten_outer_dims().rearrange("(p t) a -> p t a", t=ROW_TILES)
        k_rows = k_rot.flatten_outer_dims().rearrange("(p t) a -> p t a", t=ROW_TILES)
        hs_rows = hidden_states.flatten_outer_dims().rearrange("(p t) k -> p t k", t=ROW_TILES)
        out_heads = out.flatten_outer_dims().rearrange("(h a) (b x) -> h (a b) x", h=H, b=2)

        warm = keep.tile([P, 1], F32)
        nc.vector.memset(warm[:], 0.0)
        nc.scalar.activation(out=warm[:], in_=warm[:], func=ACT.Exp)
        ident_bf16 = keep.tile([P, P], BF16)
        make_identity(nc, ident_bf16[:])
        ident_f32 = keep.tile([P, P], F32)
        make_identity(nc, ident_f32[:])
        bias = keep.tile([P, A], BF16)
        unread = psum.tile([P, BANK], F32, tag="sc", bufs=2, name="unread")
        for i in range(16):
            nc.tensor.matmul(out=unread[:, 0:P], lhsT=ident_bf16[:], rhs=ident_bf16[:], start=True, stop=True)

        kT = keep.tile([P, ROW_TILES * A], BF16)
        hs_codes = keep.tile([P, PASSES * S], U32, align_bytes=64)
        hs_scales = keep.tile([P, PASSES * S], U8, align_bytes=64)
        p_codes = keep.tile([P, H * S], U32, align_bytes=64)
        p_scales = keep.tile([P, H * S], U8, align_bytes=64)
        v_codes = keep.tile([P, A], U32, align_bytes=64)
        v_scales = keep.tile([P, A], U8, align_bytes=64)

        stream = [("hs", i) for i in range(HS_STEPS)] + [("w", h, half) for h in range(H) for half in range(2)]

        def load_step(k, pieces=1):
            raw = work.tile([P, RAW], BF16, tag="raw", bufs=AHEAD + 1)
            step = stream[k]
            if step[0] == "hs":
                width = RAW // ROW_TILES
                view = hs_rows[:, :, step[1] * width : (step[1] + 1) * width]
                dst = raw[:].rearrange("p (t c) -> p t c", t=ROW_TILES)
                piece = width // pieces
                for i in range(pieces):
                    cols = slice(i * piece, (i + 1) * piece)
                    nc.sync.dma_start(out=dst[:, :, cols], in_=view[:, :, cols])
            else:
                h, half = step[1:]
                nc.sync.dma_start(out=raw[:], in_=Wv[h * HD : (h + 1) * HD, half * RAW : (half + 1) * RAW])
            return raw

        def load_rows(rows, t):
            raw = work.tile([P, A], BF16, tag="qk_raw", bufs=3)
            nc.sync.dma_start(out=raw[:], in_=rows[:, t, :])
            return raw

        def transpose_rows(raw, dst, copy=None):
            bank = psum.tile([P, A], BF16, tag="tp", bufs=4)
            for h in range(H):
                nc.tensor.transpose(bank[:, h * P : (h + 1) * P], raw[:, h * HD : (h + 1) * HD], ident_bf16[:])
            if copy is None:
                return dst, bank
            copy(out=dst, in_=bank[:])

        def transpose_step(k, raw, late, grouped, banks):
            words = raw[:].bitcast(F32)
            for b in banks:
                bank = psum.tile([P, BANK], F32, tag="tp", bufs=4)
                for a in range(2):
                    for u in range(2):
                        if stream[k][0] == "hs":
                            blk = (2 * (b % 2) + a) * 4 + (b // 2) * 2 + u
                        else:
                            blk = 4 * b + 2 * a + u
                        slot = (2 * a + u) * P
                        nc.tensor.transpose(bank[:, slot : slot + P], words[:, blk * P : (blk + 1) * P], ident_f32[:])
                move = dict(
                    out=grouped[:, b * BANK : (b + 1) * BANK].rearrange("p (a r u) -> p a r u", a=2, u=2),
                    in_=bank[:].rearrange("p (a u r) -> p a r u", a=2, u=2),
                )
                if b < late:
                    nc.scalar.copy(**move)
                else:
                    moves.append(move)

        moves = []
        weights = {}

        def quantise_step(k, grouped):
            step = stream[k]
            if step[0] == "hs":
                codes, scales, first = hs_codes, hs_scales, step[1] * (RAW // PACK)
            else:
                codes = work.tile([P, RAW // PACK], U32, tag="w_codes", bufs=4, align_bytes=64, name="w_codes")
                scales = work.tile([P, RAW // PACK], U8, tag="w_scales", bufs=4, align_bytes=64, name="w_scales")
                weights[step[1:]] = (codes, scales)
                first = 0
            cols = slice(first, first + RAW // PACK)
            nc.vector.quantize_mx(out=codes[:, cols].bitcast(FP8X4), scales=scales[:, cols], in_=grouped[:].bitcast(BF16))

        accs = {}

        def project(h, t):
            if t == 0:
                accs[h] = psum.tile([P, BANK], F32, tag="acc", bufs=2, name="acc")
            for c in range(PASSES):
                half, i = divmod(c, PASSES // 2)
                w_codes, w_scales = weights[h, half]
                hs_cols = slice(c * S + t * P, c * S + (t + 1) * P)
                w_cols = slice(i * HD, (i + 1) * HD)
                nc.tensor.matmul_mx(
                    out=accs[h][:, t * HD : (t + 1) * HD],
                    lhsT=hs_codes[:, hs_cols].bitcast(FP8X4),
                    lhsT_scale=hs_scales[:, hs_cols],
                    rhs=w_codes[:, w_cols].bitcast(FP8X4),
                    rhs_scale=w_scales[:, w_cols],
                    start=(c == 0),
                    stop=(c == PASSES - 1),
                )

        def add_bias(h):
            v_grouped = work.tile([P, HD * PACK], BF16, tag="v_grouped", align_bytes=64, name="v_grouped")
            nc.vector.tensor_tensor(
                out=v_grouped[:].rearrange("p (d t) -> p d t", t=PACK),
                in0=accs[h][:].rearrange("p (t d) -> p d t", t=PACK),
                in1=bias[:, h * HD : (h + 1) * HD].unsqueeze(2).to_broadcast([P, HD, PACK]),
                op=ALU.add,
            )
            return v_grouped

        def quantise_v(h, v_grouped):
            cols = slice(h * HD, (h + 1) * HD)
            nc.vector.quantize_mx(out=v_codes[:, cols].bitcast(FP8X4), scales=v_scales[:, cols], in_=v_grouped[:])

        score_banks = {}
        qT = {}
        expd = {}
        totals = {}
        twos = {}

        def scores(unit):
            it, t = divmod(unit, ROW_TILES)
            score_banks[unit] = [psum.tile([P, BANK], F32, tag="sc", bufs=2, name="sc") for g in range(2)]
            for g in range(2):
                for h in range(H):
                    first = h * P + g * HALF
                    nc.tensor.matmul(
                        out=score_banks[unit][g][:, h * HALF : (h + 1) * HALF],
                        lhsT=kT[:, t * A + h * HD : t * A + (h + 1) * HD],
                        rhs=qT[it][:, first : first + HALF],
                        start=True,
                        stop=True,
                    )

        def unit_cells(it, t):
            return expd[it][:].rearrange("p (h c t i) -> p t h c i", h=H, t=ROW_TILES, i=RUN)[:, t]

        def subtract_max(unit):
            it, t = divmod(unit, ROW_TILES)
            banks = score_banks[unit]
            top = work.tile([P, P], F32, tag="top")
            for g in range(2):
                nc.vector.tensor_reduce(
                    out=top[:, g * HALF : (g + 1) * HALF],
                    in_=banks[g][:].rearrange("p (h i) -> p i h", h=H),
                    axis=AXIS.X,
                    op=ALU.max,
                )
            if t == 0:
                expd[it] = work.tile([P, ROW_TILES * A], F32, tag="expd", bufs=4, name="expd")
            cells = unit_cells(it, t)
            for g in range(2):
                nc.vector.tensor_tensor(
                    out=cells[:, :, g * RUNS // 2 : (g + 1) * RUNS // 2],
                    in0=banks[g][:].rearrange("p (h c i) -> p h c i", h=H, i=RUN),
                    in1=top[:, g * HALF : (g + 1) * HALF]
                    .rearrange("p (c i) -> p c i", i=RUN)
                    .unsqueeze(1)
                    .to_broadcast([P, H, RUNS // 2, RUN]),
                    op=ALU.subtract,
                )

        def exp_and_sum(unit):
            it, t = divmod(unit, ROW_TILES)
            batch, member = BATCH_OF[it]
            cells = unit_cells(it, t).rearrange("p h c i -> p (h c) i")
            nc.scalar.activation(out=cells, in_=cells, func=ACT.Exp)
            if member == 0 and t == 0:
                totals[batch] = work.tile([P, len(BATCHES[batch]) * S], F32, tag="totals%d" % batch, bufs=1, name="totals")
            part = work.tile([P, 4 * P], F32, tag="part", bufs=1)
            sums = totals[batch][:, member * S : (member + 1) * S].rearrange("p (c t i) -> p t c i", t=ROW_TILES, i=RUN)[:, t - 1 : t + 1]
            fours = part[:, 0 : 4 * P].rearrange("p (c i) -> p c i", i=RUN)
            half = RUNS * H // 2
            nc.gpsimd.tensor_tensor(out=fours, in0=cells[:, 0:half], in1=cells[:, half : 2 * half], op=ALU.add)
            if t % 2 == 0:
                twos[it] = work.tile([P, 4 * P], F32, tag="twos", bufs=2, name="twos")
            at = (t % 2) * 2 * P
            nc.gpsimd.tensor_tensor(out=twos[it][:, at : at + 2 * P], in0=part[:, 0 : 2 * P], in1=part[:, 2 * P : 4 * P], op=ALU.add)
            if t % 2 == 0:
                return None
            halves = twos[it][:].rearrange("p (u f c i) -> p u f c i", u=2, f=2, i=RUN)
            return dict(out=sums, in0=halves[:, :, 0], in1=halves[:, :, 1], op=ALU.add)

        def log_sums(batch):
            nc.scalar.activation(out=totals[batch][:], in_=totals[batch][:], func=ACT.Ln)

        def invert_sums(batch):
            nc.scalar.activation(out=totals[batch][:], in_=totals[batch][:], func=ACT.Exp, scale=-1.0)

        def normalise(it, h, heads, p_grouped, at):
            batch, member = BATCH_OF[it]
            nc.vector.tensor_tensor(
                out=p_grouped[:, at * S : (at + heads) * S].rearrange("p (h c i t) -> p h c t i", h=heads, i=RUN, t=PACK),
                in0=expd[it][:, h * S : (h + heads) * S].rearrange("p (h c t i) -> p h c t i", h=heads, i=RUN, t=PACK),
                in1=totals[batch][:, member * S : (member + 1) * S]
                .rearrange("p (c t i) -> p c t i", t=PACK, i=RUN)
                .unsqueeze(1)
                .to_broadcast([P, heads, RUNS, PACK, RUN]),
                op=ALU.mult,
            )

        def quantise_probs(it, heads, p_grouped):
            first = it * A + heads[0] * P
            cols = slice(first, first + len(heads) * P)
            nc.vector.quantize_mx(out=p_codes[:, cols].bitcast(FP8X4), scales=p_scales[:, cols], in_=p_grouped[:])

        def attend(h, copy):
            acc = psum.tile([P, BANK], F32, tag="sc", bufs=2, name="attended")
            for it in range(ROW_TILES):
                p_cols = slice(it * A + h * P, it * A + (h + 1) * P)
                v_cols = slice(h * HD, (h + 1) * HD)
                nc.tensor.matmul_mx(
                    out=acc[:, it * HD : (it + 1) * HD],
                    lhsT=p_codes[:, p_cols].bitcast(FP8X4),
                    lhsT_scale=p_scales[:, p_cols],
                    rhs=v_codes[:, v_cols].bitcast(FP8X4),
                    rhs_scale=v_scales[:, v_cols],
                    start=True,
                    stop=True,
                )
            result = work.tile([P, BANK], F32, tag="result", bufs=4)
            copy(out=result[:], in_=acc[:])
            nc.sync.dma_start(out=out_heads[h], in_=result[:])

        raws = {}
        k_raw = {}
        q_raw = {}
        k_raw[0] = load_rows(k_rows, 0)
        q_raw[0] = load_rows(q_rows, 0)
        k_raw[1] = load_rows(k_rows, 1)
        raws[0] = load_step(0)
        transpose_rows(k_raw[0], kT[:, 0:A], nc.scalar.copy)
        qT[0] = work.tile([P, A], BF16, tag="qT", name="qT")
        transpose_rows(q_raw[0], qT[0][:], nc.scalar.copy)
        k_raw[2] = load_rows(k_rows, 2)
        raws[1] = load_step(1)
        transpose_rows(k_raw[1], kT[:, A : 2 * A], nc.scalar.copy)
        k_raw[3] = load_rows(k_rows, 3)

        UNIT_AT = list(range(UNITS))
        GROUPS = ((0, 1), (2, 3), (4, 5), (6, 7))
        last_unit = UNIT_AT[-1]
        batch_end = [UNIT_AT[(its[-1] + 1) * ROW_TILES - 1] for its in BATCHES]
        grouped = {}
        jobs = []
        biasing = []
        quantising = []
        chunks = []
        filled = {}
        to_quantise = []
        probs_ready = {}
        v_ready = set()
        attended = 0
        to_exp = []
        adds = []
        for k in range(STEPS + 5):
            if k + AHEAD < STEPS:
                raws[k + AHEAD] = load_step(k + AHEAD)
            units = [u for u in range(UNITS) if UNIT_AT[u] == k]
            for it in range(1, ROW_TILES):
                if k == max(1, UNIT_AT[it * ROW_TILES] - 4):
                    q_raw[it] = load_rows(q_rows, it)
            if k == HS_STEPS + 1:
                nc.sync.dma_start(out=bias[:], in_=bv.partition_broadcast(P))
            if 0 < k <= STEPS:
                quantise_step(k - 1, grouped[k - 1])
                if stream[k - 1][0] == "w" and stream[k - 1][2] == 1:
                    h = stream[k - 1][1]
                    jobs += [(k, h, 0), (k, h, 1), (k + 1 - (k == STEPS), h, 2), (k + 1 - (k == STEPS), h, 3)]
            for h, v_grouped in quantising:
                quantise_v(h, v_grouped)
                v_ready.add(h)
            quantising = []
            adds_now = adds
            adds = []
            for u in to_exp:
                adds.append(exp_and_sum(u))
            to_exp = units
            if k < STEPS:
                grouped[k] = work.tile([P, RAW // 2], F32, tag="grouped", bufs=2, align_bytes=64, name="grouped")
                transpose_step(k, raws[k], 2 if k == batch_end[0] + 3 else 4, grouped[k], range(1))
            if units:
                scores(units[0])
            if k < STEPS:
                transpose_step(k, raws[k], 2 if k == batch_end[0] + 3 else 4, grouped[k], range(1, 4))
            for b, its in enumerate(BATCHES):
                if k == batch_end[b] + 3:
                    log_sums(b)
                if k == batch_end[b] + 5:
                    invert_sums(b)
                    for heads in GROUPS:
                        for it in its:
                            for i in range(0, len(heads), 2):
                                chunks.append((it, heads, i, k + 1))
            turned = []
            for u in range(2, UNITS):
                it, t = divmod(u, ROW_TILES)
                if UNIT_AT[u] - 2 == k and (it == 0 or t == 0):
                    if it == 0:
                        raw, dst = k_raw[t], kT[:, t * A : (t + 1) * A]
                    else:
                        qT[it] = work.tile([P, A], BF16, tag="qT", name="qT")
                        raw, dst = q_raw[it], qT[it][:]
                    if it == 0 and t == 3 or it == 3:
                        turned.append(transpose_rows(raw, dst))
                    else:
                        transpose_rows(raw, dst, nc.scalar.copy)
            for i, u in enumerate(units):
                if i > 0:
                    scores(u)
                subtract_max(u)
            for dst, bank in turned:
                nc.vector.tensor_copy(out=dst, in_=bank[:])
            for last in adds_now:
                if last is not None:
                    nc.vector.tensor_tensor(**last)
            for move in moves:
                nc.vector.tensor_copy(**move)
            moves.clear()
            for it, heads, p_grouped in to_quantise:
                quantise_probs(it, heads, p_grouped)
                probs_ready[heads] = probs_ready.get(heads, 0) + 1
            to_quantise = []
            for h in biasing:
                quantising.append((h, add_bias(h)))
            biasing = []
            room = 2 if k > last_unit + 1 else (1 if k > last_unit else 0)
            while room > 0 and chunks and chunks[0][3] <= k:
                it, heads, i, ready = chunks.pop(0)
                count = min(2, len(heads))
                if i == 0:
                    filled[it] = work.tile([P, len(heads) * S], BF16, tag="p_grouped", bufs=2, align_bytes=64, name="p_grouped")
                normalise(it, heads[i], count, filled[it], i)
                if i + count == len(heads):
                    to_quantise.append((it, heads, filled[it]))
                room -= 1
            now = [j for j in jobs if j[0] <= k]
            jobs = [j for j in jobs if j[0] > k]
            for due, h, t in now:
                project(h, t)
                if t == ROW_TILES - 1:
                    biasing.append(h)
            if k > STEPS:
                for h, v_grouped in quantising:
                    quantise_v(h, v_grouped)
                    v_ready.add(h)
                quantising = []
            for h in range(attended, H):
                heads = [g for g in GROUPS if h in g][0]
                if h == attended and h in v_ready and probs_ready.get(heads, 0) == ROW_TILES and h < attended + 2:
                    attend(h, nc.scalar.copy)
                    attended += 1
        assert attended == H
